import numpy as np
import ml_dtypes


def mxq(x, axis, fmt="e4m3"):
    dtype, down = {"e4m3": (ml_dtypes.float8_e4m3fn, 7), "e5m2": (ml_dtypes.float8_e5m2, 14)}[fmt]
    v = np.moveaxis(np.asarray(x, np.float32).astype(ml_dtypes.bfloat16).astype(np.float64), axis, -1)
    blocks = v.reshape(v.shape[:-1] + (-1, 32))
    amax = np.abs(blocks).max(-1, keepdims=True)
    byte = np.maximum(np.where(amax > 0, np.frexp(amax)[1] - 1 + 127, 0) - down, 1)
    scale = np.exp2(byte - 127.0)
    codes = (blocks / scale).astype(np.float32).astype(dtype).astype(np.float64)
    return np.moveaxis((codes * scale).reshape(v.shape), -1, axis)


WIDE = False


def mx_kscale(k):
    if not WIDE:
        return np.ones(k)
    levels = np.array([10, -10, 5, -5, 0])
    a = np.random.permutation(np.resize(levels, k // 512 * 4)).reshape(k // 512, 4)
    idx = np.arange(k)
    return np.exp2(a[idx // 512, idx % 128 // 32])


BF16 = ml_dtypes.bfloat16


def bf(x):
    return np.asarray(x, np.float32).astype(BF16)


def f64(x):
    return np.asarray(x).astype(np.float64)


E, F, NR, XD, NG = 1024, 1024, 20, 3, 3
RC = 5.0


def silu(x):
    return x / (1.0 + np.exp(-x))


def setup_inputs():
    ks = mx_kscale(F)
    return {
        "s": bf(np.random.standard_normal((E, F)) * ks),
        "r": bf(np.random.standard_normal((E, XD)) * 2.0),
        "v": bf(np.random.standard_normal((E, XD, F))),
        "rbf_proj": bf(np.random.standard_normal((E, NG * F)) * 0.35),
        "W1": bf(np.random.standard_normal((F, F)) / np.sqrt(F) / ks[:, None]),
        "b1": bf(np.random.standard_normal(F) * 0.2),
        "W2": bf(np.random.standard_normal((F, NG * F)) / np.sqrt(F)),
        "b2": bf(np.random.standard_normal(NG * F) * 0.1),
        "br": bf(np.random.standard_normal(NG * F) * 0.05),
    }


def reference(s, r, v, rbf_proj, W1, b1, W2, b2, br):
    r = f64(r)
    d = np.sqrt(np.sum(r * r, axis=-1, keepdims=True))
    fcut = 0.5 * (np.cos(np.pi * d / RC) + 1.0) * (d < RC)
    h = silu((mxq(f64(s), 1, "e4m3") @ mxq(f64(W1), 0, "e4m3")) + f64(b1))
    phi = (mxq(h, 1, "e4m3") @ mxq(f64(W2), 0, "e4m3")) + f64(b2)
    wfilt = (f64(rbf_proj) + f64(br)) * fcut
    split = wfilt * phi
    wv1 = split[:, :F]
    ws = split[:, F:F + F]
    wv2 = split[:, F + F:]
    out_s = np.sum(ws, axis=0)
    unit_r = r / d
    dv = unit_r[:, :, None] * wv2[:, None, :] + wv1[:, None, :] * f64(v)
    out_v = np.sum(dv, axis=0)
    return (out_v, out_s)

@@ -1,0 +1,334 @@
+import math
+from contextlib import ExitStack
+
+import concourse.mybir as mybir
+from concourse.masks import make_identity
+
+BF16 = mybir.dt.bfloat16
+F32 = mybir.dt.float32
+U32 = mybir.dt.uint32
+U8 = mybir.dt.uint8
+FP8X4 = mybir.dt.float8_e4m3fn_x4
+ALU = mybir.AluOpType
+ACT = mybir.ActivationFunctionType
+
+P = 128
+E = 1024
+F = 1024
+XD = 3
+RC = 5.0
+ET = E // P
+JT = F // P
+PACK = 4
+K_PASS = P * PACK
+PASSES = F // K_PASS
+BANK = 512
+HALVES = E // BANK
+BLK_V1, BLK_S, BLK_V2 = 0, 1, 2
+ROW_B2, ROW_BR, ROW_B1 = 0, 32, 64
+VECTOR_SHARE = 680
+
+FLOPS = 2 * E * F * F + 2 * E * F * 3 * F
+
+
+def regroup(nc, grouped, rows, vector_cols):
+    width = rows.shape[2]
+    dst = grouped.rearrange("p (c t) -> p c t", t=PACK)
+    if vector_cols > 0:
+        nc.vector.tensor_copy(
+            out=dst[:, 0:vector_cols, :].rearrange("p (c i) t -> p c t i", i=4),
+            in_=rows[:, :, 0:vector_cols].rearrange("p t (c i) -> p c t i", i=4),
+        )
+    if vector_cols < width:
+        nc.scalar.copy(
+            out=dst[:, vector_cols:width, :].rearrange("p (c i) t -> p c t i", i=4),
+            in_=rows[:, :, vector_cols:width].rearrange("p t (c i) -> p c t i", i=4),
+        )
+
+
+def quantise(nc, grouped, codes, scales):
+    nc.vector.quantize_mx(out=codes.bitcast(FP8X4), scales=scales, in_=grouped)
+
+
+def mx_product(nc, acc, a_codes, a_scales, a_cols, b_codes, b_scales, b_cols):
+    for g in range(PASSES):
+        nc.tensor.matmul_mx(
+            out=acc,
+            lhsT=a_codes[:, g, a_cols].bitcast(FP8X4),
+            lhsT_scale=a_scales[:, g, a_cols],
+            rhs=b_codes[:, g, b_cols].bitcast(FP8X4),
+            rhs_scale=b_scales[:, g, b_cols],
+            start=(g == 0),
+            stop=(g == PASSES - 1),
+        )
+
+
+def tile_message_pa_kernel(tc, s, r, v, rbf_proj, W1, b1, W2, b2, br, out_0, out_1):
+    nc = tc.nc
+    with ExitStack() as ctx:
+        keep = ctx.enter_context(tc.tile_pool(name="keep", bufs=1))
+        overlay = ctx.enter_context(tc.tile_pool(name="overlay", bufs=1))
+        stage = ctx.enter_context(tc.tile_pool(name="stage", bufs=2))
+        psum = ctx.enter_context(tc.psum_pool(name="psum", bufs=1))
+
+        ident_bf = keep.tile([P, P], BF16)
+        make_identity(nc, ident_bf[:])
+        ident_f = keep.tile([P, P], F32)
+        make_identity(nc, ident_f[:])
+
+        r_bf = keep.tile([P, ET, XD], BF16)
+        nc.sync.dma_start(out=r_bf[:], in_=r.rearrange("(p t) c -> p t c", t=ET))
+        bias_rows = keep.tile([P, P], BF16)
+        nc.vector.memset(bias_rows[:], 0.0)
+        nc.sync.dma_start(out=bias_rows[ROW_B2 : ROW_B2 + 3 * JT, :], in_=b2.rearrange("(a c) -> a c", c=P))
+        nc.sync.dma_start(out=bias_rows[ROW_BR : ROW_BR + 3 * JT, :], in_=br.rearrange("(a c) -> a c", c=P))
+        nc.sync.dma_start(out=bias_rows[ROW_B1 : ROW_B1 + JT, :], in_=b1.rearrange("(a c) -> a c", c=P))
+
+        s_raw = overlay.tile([P, ET, F], BF16, offset=0)
+        s_view = s.rearrange("(p t) k -> p t k", t=ET)
+        for a in range(0, ET, 2):
+            nc.sync.dma_start(out=s_raw[:, a : a + 2, :], in_=s_view[:, a : a + 2, :])
+        w1_raw = overlay.tile([P, PASSES, PACK, F], BF16, offset=16384)
+        for g in range(PASSES):
+            nc.sync.dma_start(
+                out=w1_raw[:, g].rearrange("q (u e) c -> q u (e c)", u=2),
+                in_=W1[g * K_PASS : (g + 1) * K_PASS, :].rearrange("(u q e) c -> q u (e c)", u=2, e=2),
+            )
+        h_lin = overlay.tile([P, PASSES, PACK, E], BF16, offset=32768)
+        s_codes = overlay.tile([P, PASSES, E], U32, offset=49152, align_bytes=64)
+        w1_codes = overlay.tile([P, PASSES, F], U32, offset=57344, align_bytes=64)
+        s_scales = overlay.tile([P, PASSES, E], U8, offset=65536, align_bytes=64)
+        w1_scales = overlay.tile([P, PASSES, F], U8, offset=67584, align_bytes=64)
+
+        h_codes = keep.tile([P, PASSES, E], U32, align_bytes=64)
+        h_scales = keep.tile([P, PASSES, E], U8, align_bytes=64)
+        w2_codes = keep.tile([P, PASSES, 3 * F], U32, align_bytes=64)
+        w2_scales = keep.tile([P, PASSES, 3 * F], U8, align_bytes=64)
+
+        def load_w2_block(blk):
+            chunks = []
+            for g in range(PASSES):
+                w2_raw = stage.tile([P, PACK, F], BF16, tag="w2_raw")
+                nc.sync.dma_start(
+                    out=w2_raw[:],
+                    in_=W2[g * K_PASS : (g + 1) * K_PASS, blk * F : (blk + 1) * F].rearrange("(t p) n -> p t n", p=P),
+                )
+                chunks.append(w2_raw)
+            return chunks
+
+        def quantise_w2_block(blk, chunks, vector_cols):
+            cols = slice(blk * F, (blk + 1) * F)
+            for g in range(PASSES):
+                grouped = stage.tile([P, PACK * F], BF16, tag="grouped", bufs=3, align_bytes=64)
+                regroup(nc, grouped[:], chunks[g][:], vector_cols)
+                quantise(nc, grouped[:], w2_codes[:, g, cols], w2_scales[:, g, cols])
+
+        def load_rbf_block(blk, rbf_tile):
+            nc.sync.dma_start(
+                out=rbf_tile[:],
+                in_=rbf_proj[:, blk * F : (blk + 1) * F].rearrange("(p t) j -> p t j", t=ET),
+            )
+
+        w2_v2_chunks = load_w2_block(BLK_V2)
+        br_bc = keep.tile([P, F], BF16)
+        nc.sync.dma_start(out=br_bc[:], in_=br[BLK_V2 * F : (BLK_V2 + 1) * F].partition_broadcast(P))
+        b2_bc = keep.tile([P, F], BF16)
+        nc.sync.dma_start(out=b2_bc[:], in_=b2[BLK_V2 * F : (BLK_V2 + 1) * F].partition_broadcast(P))
+        rbf_v2 = keep.tile([P, ET, F], BF16)
+        load_rbf_block(BLK_V2, rbf_v2)
+
+        bias_ps = psum.tile([P, P], BF16, tag="tr", bufs=5)
+        nc.tensor.transpose(bias_ps[:], bias_rows[:], ident_bf[:])
+        bias_cols = keep.tile([P, P], F32)
+        nc.vector.tensor_copy(out=bias_cols[:], in_=bias_ps[:])
+
+        r32 = keep.tile([P, ET, XD], F32)
+        nc.vector.tensor_copy(out=r32[:], in_=r_bf[:])
+        r_sq = keep.tile([P, ET, XD], F32)
+        nc.vector.tensor_tensor(out=r_sq[:], in0=r32[:], in1=r32[:], op=ALU.mult)
+        d_sq = keep.tile([P, ET], F32)
+        nc.vector.tensor_reduce(out=d_sq[:], in_=r_sq[:], axis=mybir.AxisListType.X, op=ALU.add)
+        dist = keep.tile([P, ET], F32)
+        nc.scalar.activation(out=dist[:], in_=d_sq[:], func=ACT.Sqrt)
+        inv_d = keep.tile([P, ET], F32)
+        nc.vector.reciprocal(out=inv_d[:], in_=dist[:])
+        d_clip = keep.tile([P, ET], F32)
+        nc.vector.tensor_scalar_min(out=d_clip[:], in0=dist[:], scalar1=RC)
+        sin_d = keep.tile([P, ET], F32)
+        nc.scalar.activation(out=sin_d[:], in_=d_clip[:], func=ACT.Sin, scale=math.pi / (2.0 * RC))
+        inside = keep.tile([P, ET], F32)
+        nc.vector.tensor_single_scalar(out=inside[:], in_=dist[:], scalar=RC, op=ALU.is_lt)
+        fcut = keep.tile([P, ET], F32)
+        nc.vector.tensor_tensor(out=fcut[:], in0=sin_d[:], in1=sin_d[:], op=ALU.mult)
+        nc.vector.tensor_scalar(out=fcut[:], in0=fcut[:], scalar1=-1.0, scalar2=1.0, op0=ALU.mult, op1=ALU.add)
+        nc.vector.tensor_tensor(out=fcut[:], in0=fcut[:], in1=inside[:], op=ALU.mult)
+        fcut_over_d = keep.tile([P, ET], F32)
+        nc.vector.tensor_tensor(out=fcut_over_d[:], in0=fcut[:], in1=inv_d[:], op=ALU.mult)
+        edge_w = keep.tile([P, ET, P], F32)
+        nc.vector.memset(edge_w[:], 0.0)
+        nc.vector.tensor_tensor(
+            out=edge_w[:, :, 0:XD],
+            in0=r32[:],
+            in1=fcut_over_d[:].unsqueeze(2).to_broadcast([P, ET, XD]),
+            op=ALU.mult,
+        )
+        fcut_rep = stage.tile([P, ET, P], F32, tag="scratch", bufs=1)
+        nc.vector.tensor_copy(out=fcut_rep[:], in_=fcut[:].unsqueeze(2).to_broadcast([P, ET, P]))
+        fcut_bc = keep.tile([P, E], F32)
+        for eh in range(HALVES):
+            rep_ps = psum.tile([P, BANK], F32, tag="tr", bufs=5)
+            for i in range(BANK // P):
+                nc.tensor.transpose(rep_ps[:, i * P : (i + 1) * P], fcut_rep[:, eh * (BANK // P) + i, :], ident_f[:])
+            nc.vector.tensor_copy(out=fcut_bc[:, eh * BANK : (eh + 1) * BANK], in_=rep_ps[:])
+
+        s_words = s_raw[:].bitcast(F32)
+        s_grouped = []
+        for g in range(PASSES):
+            grouped = stage.tile([P, PACK * E], BF16, tag="grouped", bufs=3, align_bytes=64, name="s_grouped%d" % g)
+            s_grouped.append(grouped)
+        for tp in range(ET // 2):
+            for g in range(PASSES):
+                s_ps = psum.tile([P, 2, 2 * P], F32, tag="tr", bufs=5)
+                for u in range(2):
+                    for i in range(2):
+                        w0 = g * (K_PASS // 2) + u * P
+                        nc.tensor.transpose(s_ps[:, u, i * P : (i + 1) * P], s_words[:, 2 * tp + i, w0 : w0 + P], ident_f[:])
+                dst = s_grouped[g][:].bitcast(F32).rearrange("p (e u) -> p e u", u=2)
+                dst = dst[:, tp * 2 * P : (tp + 1) * 2 * P, :]
+                if g == 0:
+                    nc.vector.tensor_copy(out=dst, in_=s_ps[:].rearrange("p u e -> p e u"))
+                else:
+                    nc.scalar.copy(out=dst, in_=s_ps[:].rearrange("p u e -> p e u"))
+        for g in range(PASSES):
+            quantise(nc, s_grouped[g][:], s_codes[:, g, :], s_scales[:, g, :])
+
+        for g in range(PASSES):
+            grouped = stage.tile([P, PACK * F], BF16, tag="grouped", bufs=3, align_bytes=64)
+            regroup(nc, grouped[:], w1_raw[:, g], VECTOR_SHARE)
+            quantise(nc, grouped[:], w1_codes[:, g, :], w1_scales[:, g, :])
+        quantise_w2_block(BLK_V2, w2_v2_chunks, VECTOR_SHARE)
+
+        for eh in range(HALVES):
+            edges = slice(eh * BANK, (eh + 1) * BANK)
+            for g2 in range(PASSES):
+                for t in range(PACK):
+                    ft = g2 * PACK + t
+                    h_ps = psum.tile([P, BANK], F32, tag="phi", bufs=3)
+                    mx_product(nc, h_ps[:], w1_codes, w1_scales, slice(ft * P, (ft + 1) * P), s_codes, s_scales, edges)
+                    nc.scalar.activation(
+                        out=h_lin[:, g2, t, edges], in_=h_ps[:], func=ACT.Silu,
+                        bias=bias_cols[:, ROW_B1 + ft : ROW_B1 + ft + 1], scale=1.0,
+                    )
+                grouped = stage.tile([P, PACK * BANK], BF16, tag="grouped", bufs=3, align_bytes=64)
+                regroup(nc, grouped[:], h_lin[:, g2, :, edges], BANK)
+                quantise(nc, grouped[:], h_codes[:, g2, edges], h_scales[:, g2, edges])
+
+        w2_s_chunks = load_w2_block(BLK_S)
+        rbf_s = keep.tile([P, ET, F], BF16)
+        load_rbf_block(BLK_S, rbf_s)
+        quantise_w2_block(BLK_S, w2_s_chunks, 0)
+        w2_v1_chunks = load_w2_block(BLK_V1)
+        rbf_v1 = overlay.tile([P, ET, F], BF16, offset=49152)
+        load_rbf_block(BLK_V1, rbf_v1)
+        v_sb = overlay.tile([P, ET, XD, F], BF16, offset=0)
+        v_view = v.rearrange("(p t) c j -> p t c j", t=ET)
+        for a in range(0, ET, 2):
+            nc.sync.dma_start(out=v_sb[:, a : a + 2], in_=v_view[:, a : a + 2])
+        quantise_w2_block(BLK_V1, w2_v1_chunks, 0)
+
+        v2_acc = []
+        for jh in range(F // BANK):
+            acc = psum.tile([P, BANK], F32, tag="tr", bufs=5, name="v2_acc%d" % jh)
+            v2_acc.append(acc)
+        for t in range(ET):
+            filt = stage.tile([P, F], F32, tag="filt", bufs=4)
+            nc.gpsimd.tensor_tensor(out=filt[:], in0=rbf_v2[:, t, :], in1=br_bc[:], op=ALU.add)
+            for jh in range(F // BANK):
+                cols = slice(jh * BANK, (jh + 1) * BANK)
+                phi_ps = psum.tile([P, BANK], F32, tag="phi", bufs=3)
+                mx_product(
+                    nc, phi_ps[:], h_codes, h_scales, slice(t * P, (t + 1) * P),
+                    w2_codes, w2_scales, slice(BLK_V2 * F + jh * BANK, BLK_V2 * F + (jh + 1) * BANK),
+                )
+                phi_b = stage.tile([P, BANK], F32, tag="phi_b")
+                nc.vector.tensor_tensor(out=phi_b[:], in0=phi_ps[:], in1=b2_bc[:, cols], op=ALU.add)
+                gate = stage.tile([P, BANK], F32, tag="gate", bufs=3)
+                nc.vector.tensor_tensor(out=gate[:], in0=phi_b[:], in1=filt[:, cols], op=ALU.mult)
+                nc.tensor.matmul(out=v2_acc[jh][:], lhsT=edge_w[:, t, :], rhs=gate[:], start=(t == 0), stop=(t == ET - 1))
+        v2_rows = stage.tile([P, F], F32, tag="scratch", bufs=1)
+        res_v2 = keep.tile([P, XD, JT], F32)
+        for jh in range(F // BANK):
+            nc.vector.tensor_copy(out=v2_rows[:, jh * BANK : (jh + 1) * BANK], in_=v2_acc[jh][:])
+        for jh in range(F // BANK):
+            turn_ps = psum.tile([P, BANK // P, P], F32, tag="tr", bufs=5)
+            for i in range(BANK // P):
+                j0 = jh * BANK + i * P
+                nc.tensor.transpose(turn_ps[:, i, :], v2_rows[:, j0 : j0 + P], ident_f[:])
+            nc.vector.tensor_copy(
+                out=res_v2[:, :, jh * (BANK // P) : (jh + 1) * (BANK // P)],
+                in_=turn_ps[:, :, 0:XD].rearrange("p i c -> p c i"),
+            )
+
+        def filter_tile(blk, jt, rbf_tile):
+            rbf_ps = psum.tile([P, E], BF16, tag="tr", bufs=5)
+            for t in range(ET):
+                nc.tensor.transpose(rbf_ps[:, t * P : (t + 1) * P], rbf_tile[:, t, jt * P : (jt + 1) * P], ident_bf[:])
+            filt = stage.tile([P, E], F32, tag="filt", bufs=4)
+            col = ROW_BR + blk * JT + jt
+            nc.scalar.activation(out=filt[:], in_=rbf_ps[:], func=ACT.Identity, bias=bias_cols[:, col : col + 1], scale=1.0)
+            nc.gpsimd.tensor_tensor(out=filt[:], in0=filt[:], in1=fcut_bc[:], op=ALU.mult)
+            return filt
+
+        def phi_tile(blk, jt, eh):
+            phi_ps = psum.tile([P, BANK], F32, tag="phi", bufs=3)
+            j0 = blk * F + jt * P
+            mx_product(
+                nc, phi_ps[:], w2_codes, w2_scales, slice(j0, j0 + P),
+                h_codes, h_scales, slice(eh * BANK, (eh + 1) * BANK),
+            )
+            return phi_ps
+
+        res_s = keep.tile([P, JT, HALVES], F32)
+        res_v1 = keep.tile([P, XD, JT], F32)
+        next_filters = (filter_tile(BLK_S, 0, rbf_s), filter_tile(BLK_V1, 0, rbf_v1))
+        for jt in range(JT):
+            filt_s, filt_v1 = next_filters
+            if jt + 1 < JT:
+                next_filters = (filter_tile(BLK_S, jt + 1, rbf_s), filter_tile(BLK_V1, jt + 1, rbf_v1))
+            col = ROW_B2 + BLK_S * JT + jt
+            for eh in range(HALVES):
+                phi_ps = phi_tile(BLK_S, jt, eh)
+                nc.vector.scalar_tensor_tensor(
+                    out=filt_s[:, eh * BANK : (eh + 1) * BANK], in0=phi_ps[:], scalar=bias_cols[:, col : col + 1],
+                    in1=filt_s[:, eh * BANK : (eh + 1) * BANK], op0=ALU.add, op1=ALU.mult,
+                    accum_out=res_s[:, jt, eh : eh + 1],
+                )
+            col = ROW_B2 + BLK_V1 * JT + jt
+            gate = stage.tile([P, E], F32, tag="gate_t")
+            for eh in range(HALVES):
+                phi_ps = phi_tile(BLK_V1, jt, eh)
+                nc.vector.scalar_tensor_tensor(
+                    out=gate[:, eh * BANK : (eh + 1) * BANK], in0=phi_ps[:], scalar=bias_cols[:, col : col + 1],
+                    in1=filt_v1[:, eh * BANK : (eh + 1) * BANK], op0=ALU.add, op1=ALU.mult,
+                )
+            for c in range(XD):
+                v_ps = psum.tile([P, E], BF16, tag="tr", bufs=5)
+                for t in range(ET):
+                    nc.tensor.transpose(v_ps[:, t * P : (t + 1) * P], v_sb[:, t, c, jt * P : (jt + 1) * P], ident_bf[:])
+                nc.vector.scalar_tensor_tensor(
+                    out=filt_v1[:], in0=v_ps[:], scalar=1.0, in1=gate[:], op0=ALU.mult, op1=ALU.mult,
+                    accum_out=res_v1[:, c, jt : jt + 1],
+                )
+
+        res = keep.tile([P, P], F32)
+        nc.vector.memset(res[:], 0.0)
+        nc.vector.tensor_tensor(
+            out=res[:, 0 : XD * JT].rearrange("p (c j) -> p c j", c=XD), in0=res_v1[:], in1=res_v2[:], op=ALU.add,
+        )
+        nc.vector.tensor_tensor(out=res[:, XD * JT : (XD + 1) * JT], in0=res_s[:, :, 0], in1=res_s[:, :, 1], op=ALU.add)
+        res_ps = psum.tile([P, P], F32, tag="tr", bufs=5)
+        nc.tensor.transpose(res_ps[:], res[:], ident_f[:])
+        res_rows = keep.tile([P, P], F32)
+        nc.vector.tensor_copy(out=res_rows[:], in_=res_ps[:])
+        nc.sync.dma_start(out=out_0.rearrange("c (j p) -> (c j) p", p=P), in_=res_rows[0 : XD * JT, :])
+        nc.sync.dma_start(out=out_1.rearrange("(j p) -> j p", p=P), in_=res_rows[XD * JT : (XD + 1) * JT, :])

@@ -11,6 +11,7 @@ U8 = mybir.dt.uint8
 FP8X4 = mybir.dt.float8_e4m3fn_x4
 ALU = mybir.AluOpType
 ACT = mybir.ActivationFunctionType
+AXIS_X = mybir.AxisListType.X
 
 P = 128
 E = 1024
@@ -26,7 +27,17 @@ BANK = 512
 HALVES = E // BANK
 BLK_V1, BLK_S, BLK_V2 = 0, 1, 2
 ROW_B2, ROW_BR, ROW_B1 = 0, 32, 64
-VECTOR_SHARE = 680
+PARTS = 3
+VECTOR_SHARE = 344
+GPSIMD_TILES = 6
+RAW_BUFS = 3
+GROUPED_BUFS = 5
+RBF_BUFS = 5
+WORK_BUFS = 10
+TR_BUFS = 3
+PHI_BUFS = 3
+LAG_S = 2
+LAG_V1 = 5
 
 FLOPS = 2 * E * F * F + 2 * E * F * 3 * F
 
@@ -50,6 +61,16 @@ def quantise(nc, grouped, codes, scales):
     nc.vector.quantize_mx(out=codes.bitcast(FP8X4), scales=scales, in_=grouped)
 
 
+def split(nc, pool, name, value, parts, shape):
+    rest = value
+    for i, part in enumerate(parts):
+        nc.gpsimd.tensor_copy(out=part, in_=rest)
+        if i + 1 < len(parts):
+            left = pool.tile(shape, F32, name="%s_rest%d" % (name, i))
+            nc.gpsimd.tensor_tensor(out=left[:], in0=rest, in1=part, op=ALU.subtract)
+            rest = left[:]
+
+
 def mx_product(nc, acc, a_codes, a_scales, a_cols, b_codes, b_scales, b_cols):
     for g in range(PASSES):
         nc.tensor.matmul_mx(
@@ -71,216 +92,263 @@ def tile_message_pa_kernel(tc, s, r, v, rbf_proj, W1, b1, W2, b2, br, out_0, out
         stage = ctx.enter_context(tc.tile_pool(name="stage", bufs=2))
         psum = ctx.enter_context(tc.psum_pool(name="psum", bufs=1))
 
-        ident_bf = keep.tile([P, P], BF16)
-        make_identity(nc, ident_bf[:])
         ident_f = keep.tile([P, P], F32)
         make_identity(nc, ident_f[:])
+        ident_bf = keep.tile([P, P], BF16)
+        make_identity(nc, ident_bf[:])
 
         r_bf = keep.tile([P, ET, XD], BF16)
         nc.sync.dma_start(out=r_bf[:], in_=r.rearrange("(p t) c -> p t c", t=ET))
+        s_raw = overlay.tile([P, ET, F], BF16, offset=0)
+        s_view = s.rearrange("(p t) k -> p t k", t=ET)
+        EH = ET // HALVES
+
+        def load_s_half(eh):
+            nc.sync.dma_start(out=s_raw[:, eh * EH : (eh + 1) * EH, :], in_=s_view[:, eh * EH : (eh + 1) * EH, :])
+
+        load_s_half(0)
+        w1_raw = []
+        for g in range(PASSES):
+            raw = stage.tile([P, PACK, F], BF16, tag="raw", bufs=RAW_BUFS)
+            nc.sync.dma_start(
+                out=raw[:].rearrange("q (u e) c -> q u (e c)", u=2),
+                in_=W1[g * K_PASS : (g + 1) * K_PASS, :].rearrange("(u q e) c -> q u (e c)", u=2, e=2),
+            )
+            w1_raw.append(raw)
+        load_s_half(1)
         bias_rows = keep.tile([P, P], BF16)
-        nc.vector.memset(bias_rows[:], 0.0)
+        nc.gpsimd.memset(bias_rows[:], 0.0)
         nc.sync.dma_start(out=bias_rows[ROW_B2 : ROW_B2 + 3 * JT, :], in_=b2.rearrange("(a c) -> a c", c=P))
         nc.sync.dma_start(out=bias_rows[ROW_BR : ROW_BR + 3 * JT, :], in_=br.rearrange("(a c) -> a c", c=P))
         nc.sync.dma_start(out=bias_rows[ROW_B1 : ROW_B1 + JT, :], in_=b1.rearrange("(a c) -> a c", c=P))
 
-        s_raw = overlay.tile([P, ET, F], BF16, offset=0)
-        s_view = s.rearrange("(p t) k -> p t k", t=ET)
-        for a in range(0, ET, 2):
-            nc.sync.dma_start(out=s_raw[:, a : a + 2, :], in_=s_view[:, a : a + 2, :])
-        w1_raw = overlay.tile([P, PASSES, PACK, F], BF16, offset=16384)
-        for g in range(PASSES):
-            nc.sync.dma_start(
-                out=w1_raw[:, g].rearrange("q (u e) c -> q u (e c)", u=2),
-                in_=W1[g * K_PASS : (g + 1) * K_PASS, :].rearrange("(u q e) c -> q u (e c)", u=2, e=2),
-            )
-        h_lin = overlay.tile([P, PASSES, PACK, E], BF16, offset=32768)
-        s_codes = overlay.tile([P, PASSES, E], U32, offset=49152, align_bytes=64)
-        w1_codes = overlay.tile([P, PASSES, F], U32, offset=57344, align_bytes=64)
-        s_scales = overlay.tile([P, PASSES, E], U8, offset=65536, align_bytes=64)
-        w1_scales = overlay.tile([P, PASSES, F], U8, offset=67584, align_bytes=64)
+        def load_w2_block(blk):
+            chunks = []
+            for g in range(PASSES):
+                raw = stage.tile([P, PACK, F], BF16, tag="raw", bufs=RAW_BUFS)
+                nc.sync.dma_start(
+                    out=raw[:],
+                    in_=W2[g * K_PASS : (g + 1) * K_PASS, blk * F : (blk + 1) * F].rearrange("(t p) n -> p t n", p=P),
+                )
+                chunks.append(raw)
+            return chunks
 
+        def load_rbf_block(blk):
+            halves = []
+            for half in range(HALVES):
+                rbf = stage.tile([P, EH, F], BF16, tag="rbf", bufs=RBF_BUFS)
+                nc.sync.dma_start(
+                    out=rbf[:],
+                    in_=rbf_proj[:, blk * F : (blk + 1) * F].rearrange("(p t) j -> p t j", t=ET)[:, half * EH : (half + 1) * EH, :],
+                )
+                halves.append(rbf)
+            return halves
+
+        h_lin = overlay.tile([P, PASSES, PACK, E], BF16, offset=16384)
+        s_codes = overlay.tile([P, PASSES, E], U32, offset=32768, align_bytes=64)
+        w1_codes = overlay.tile([P, PASSES, F], U32, offset=40960, align_bytes=64)
+        s_scales = overlay.tile([P, PASSES, E], U8, offset=49152, align_bytes=64)
+        w1_scales = overlay.tile([P, PASSES, F], U8, offset=51200, align_bytes=64)
         h_codes = keep.tile([P, PASSES, E], U32, align_bytes=64)
         h_scales = keep.tile([P, PASSES, E], U8, align_bytes=64)
         w2_codes = keep.tile([P, PASSES, 3 * F], U32, align_bytes=64)
         w2_scales = keep.tile([P, PASSES, 3 * F], U8, align_bytes=64)
 
-        def load_w2_block(blk):
-            chunks = []
-            for g in range(PASSES):
-                w2_raw = stage.tile([P, PACK, F], BF16, tag="w2_raw")
-                nc.sync.dma_start(
-                    out=w2_raw[:],
-                    in_=W2[g * K_PASS : (g + 1) * K_PASS, blk * F : (blk + 1) * F].rearrange("(t p) n -> p t n", p=P),
-                )
-                chunks.append(w2_raw)
-            return chunks
+        w2_v2_chunks = load_w2_block(BLK_V2)
+        br_bc = keep.tile([P, F], BF16)
+        nc.sync.dma_start(out=br_bc[:], in_=br[BLK_V2 * F : (BLK_V2 + 1) * F].partition_broadcast(P))
+        rbf_v2 = load_rbf_block(BLK_V2)
+
+        def quantise_weights(raw, codes, scales, vector_cols):
+            for c0 in range(0, F, BANK):
+                grouped = stage.tile([P, PACK * BANK], BF16, tag="grouped", bufs=GROUPED_BUFS, align_bytes=64)
+                regroup(nc, grouped[:], raw[:, :, c0 : c0 + BANK], vector_cols)
+                quantise(nc, grouped[:], codes[:, c0 : c0 + BANK], scales[:, c0 : c0 + BANK])
 
         def quantise_w2_block(blk, chunks, vector_cols):
             cols = slice(blk * F, (blk + 1) * F)
             for g in range(PASSES):
-                grouped = stage.tile([P, PACK * F], BF16, tag="grouped", bufs=3, align_bytes=64)
-                regroup(nc, grouped[:], chunks[g][:], vector_cols)
-                quantise(nc, grouped[:], w2_codes[:, g, cols], w2_scales[:, g, cols])
-
-        def load_rbf_block(blk, rbf_tile):
-            nc.sync.dma_start(
-                out=rbf_tile[:],
-                in_=rbf_proj[:, blk * F : (blk + 1) * F].rearrange("(p t) j -> p t j", t=ET),
-            )
-
-        w2_v2_chunks = load_w2_block(BLK_V2)
-        br_bc = keep.tile([P, F], BF16)
-        nc.sync.dma_start(out=br_bc[:], in_=br[BLK_V2 * F : (BLK_V2 + 1) * F].partition_broadcast(P))
-        b2_bc = keep.tile([P, F], BF16)
-        nc.sync.dma_start(out=b2_bc[:], in_=b2[BLK_V2 * F : (BLK_V2 + 1) * F].partition_broadcast(P))
-        rbf_v2 = keep.tile([P, ET, F], BF16)
-        load_rbf_block(BLK_V2, rbf_v2)
-
-        bias_ps = psum.tile([P, P], BF16, tag="tr", bufs=5)
-        nc.tensor.transpose(bias_ps[:], bias_rows[:], ident_bf[:])
-        bias_cols = keep.tile([P, P], F32)
-        nc.vector.tensor_copy(out=bias_cols[:], in_=bias_ps[:])
-
-        r32 = keep.tile([P, ET, XD], F32)
-        nc.vector.tensor_copy(out=r32[:], in_=r_bf[:])
-        r_sq = keep.tile([P, ET, XD], F32)
-        nc.vector.tensor_tensor(out=r_sq[:], in0=r32[:], in1=r32[:], op=ALU.mult)
-        d_sq = keep.tile([P, ET], F32)
-        nc.vector.tensor_reduce(out=d_sq[:], in_=r_sq[:], axis=mybir.AxisListType.X, op=ALU.add)
-        dist = keep.tile([P, ET], F32)
-        nc.scalar.activation(out=dist[:], in_=d_sq[:], func=ACT.Sqrt)
-        inv_d = keep.tile([P, ET], F32)
-        nc.vector.reciprocal(out=inv_d[:], in_=dist[:])
-        d_clip = keep.tile([P, ET], F32)
-        nc.vector.tensor_scalar_min(out=d_clip[:], in0=dist[:], scalar1=RC)
-        sin_d = keep.tile([P, ET], F32)
-        nc.scalar.activation(out=sin_d[:], in_=d_clip[:], func=ACT.Sin, scale=math.pi / (2.0 * RC))
-        inside = keep.tile([P, ET], F32)
-        nc.vector.tensor_single_scalar(out=inside[:], in_=dist[:], scalar=RC, op=ALU.is_lt)
-        fcut = keep.tile([P, ET], F32)
-        nc.vector.tensor_tensor(out=fcut[:], in0=sin_d[:], in1=sin_d[:], op=ALU.mult)
-        nc.vector.tensor_scalar(out=fcut[:], in0=fcut[:], scalar1=-1.0, scalar2=1.0, op0=ALU.mult, op1=ALU.add)
-        nc.vector.tensor_tensor(out=fcut[:], in0=fcut[:], in1=inside[:], op=ALU.mult)
-        fcut_over_d = keep.tile([P, ET], F32)
-        nc.vector.tensor_tensor(out=fcut_over_d[:], in0=fcut[:], in1=inv_d[:], op=ALU.mult)
-        edge_w = keep.tile([P, ET, P], F32)
-        nc.vector.memset(edge_w[:], 0.0)
-        nc.vector.tensor_tensor(
-            out=edge_w[:, :, 0:XD],
-            in0=r32[:],
-            in1=fcut_over_d[:].unsqueeze(2).to_broadcast([P, ET, XD]),
-            op=ALU.mult,
-        )
-        fcut_rep = stage.tile([P, ET, P], F32, tag="scratch", bufs=1)
-        nc.vector.tensor_copy(out=fcut_rep[:], in_=fcut[:].unsqueeze(2).to_broadcast([P, ET, P]))
-        fcut_bc = keep.tile([P, E], F32)
-        for eh in range(HALVES):
-            rep_ps = psum.tile([P, BANK], F32, tag="tr", bufs=5)
-            for i in range(BANK // P):
-                nc.tensor.transpose(rep_ps[:, i * P : (i + 1) * P], fcut_rep[:, eh * (BANK // P) + i, :], ident_f[:])
-            nc.vector.tensor_copy(out=fcut_bc[:, eh * BANK : (eh + 1) * BANK], in_=rep_ps[:])
+                quantise_weights(chunks[g], w2_codes[:, g, cols], w2_scales[:, g, cols], vector_cols)
 
         s_words = s_raw[:].bitcast(F32)
-        s_grouped = []
-        for g in range(PASSES):
-            grouped = stage.tile([P, PACK * E], BF16, tag="grouped", bufs=3, align_bytes=64, name="s_grouped%d" % g)
-            s_grouped.append(grouped)
-        for tp in range(ET // 2):
+
+        def quantise_s_half(eh):
+            grouped = []
             for g in range(PASSES):
-                s_ps = psum.tile([P, 2, 2 * P], F32, tag="tr", bufs=5)
-                for u in range(2):
-                    for i in range(2):
-                        w0 = g * (K_PASS // 2) + u * P
-                        nc.tensor.transpose(s_ps[:, u, i * P : (i + 1) * P], s_words[:, 2 * tp + i, w0 : w0 + P], ident_f[:])
-                dst = s_grouped[g][:].bitcast(F32).rearrange("p (e u) -> p e u", u=2)
-                dst = dst[:, tp * 2 * P : (tp + 1) * 2 * P, :]
-                if g == 0:
-                    nc.vector.tensor_copy(out=dst, in_=s_ps[:].rearrange("p u e -> p e u"))
-                else:
-                    nc.scalar.copy(out=dst, in_=s_ps[:].rearrange("p u e -> p e u"))
-        for g in range(PASSES):
-            quantise(nc, s_grouped[g][:], s_codes[:, g, :], s_scales[:, g, :])
+                tile_g = stage.tile([P, PACK * BANK], BF16, tag="grouped", bufs=GROUPED_BUFS, align_bytes=64, name="s_grouped%d" % g)
+                grouped.append(tile_g)
+            for tp in range(EH // 2):
+                for g in range(PASSES):
+                    s_ps = psum.tile([P, 2, 2 * P], F32, tag="tr", bufs=TR_BUFS)
+                    for u in range(2):
+                        for i in range(2):
+                            w0 = g * (K_PASS // 2) + u * P
+                            nc.tensor.transpose(
+                                s_ps[:, u, i * P : (i + 1) * P], s_words[:, eh * EH + 2 * tp + i, w0 : w0 + P], ident_f[:]
+                            )
+                    dst = grouped[g][:].bitcast(F32).rearrange("p (e u) -> p e u", u=2)
+                    dst = dst[:, tp * 2 * P : (tp + 1) * 2 * P, :]
+                    if g == 0:
+                        nc.vector.tensor_copy(out=dst, in_=s_ps[:].rearrange("p u e -> p e u"))
+                    else:
+                        nc.scalar.copy(out=dst, in_=s_ps[:].rearrange("p u e -> p e u"))
+            edges = slice(eh * BANK, (eh + 1) * BANK)
+            for g in range(PASSES):
+                quantise(nc, grouped[g][:], s_codes[:, g, edges], s_scales[:, g, edges])
 
-        for g in range(PASSES):
-            grouped = stage.tile([P, PACK * F], BF16, tag="grouped", bufs=3, align_bytes=64)
-            regroup(nc, grouped[:], w1_raw[:, g], VECTOR_SHARE)
-            quantise(nc, grouped[:], w1_codes[:, g, :], w1_scales[:, g, :])
-        quantise_w2_block(BLK_V2, w2_v2_chunks, VECTOR_SHARE)
-
-        for eh in range(HALVES):
+        def first_product(eh):
             edges = slice(eh * BANK, (eh + 1) * BANK)
             for g2 in range(PASSES):
                 for t in range(PACK):
                     ft = g2 * PACK + t
-                    h_ps = psum.tile([P, BANK], F32, tag="phi", bufs=3)
+                    h_ps = psum.tile([P, BANK], F32, tag="phi", bufs=PHI_BUFS)
                     mx_product(nc, h_ps[:], w1_codes, w1_scales, slice(ft * P, (ft + 1) * P), s_codes, s_scales, edges)
                     nc.scalar.activation(
                         out=h_lin[:, g2, t, edges], in_=h_ps[:], func=ACT.Silu,
                         bias=bias_cols[:, ROW_B1 + ft : ROW_B1 + ft + 1], scale=1.0,
                     )
-                grouped = stage.tile([P, PACK * BANK], BF16, tag="grouped", bufs=3, align_bytes=64)
+                grouped = stage.tile([P, PACK * BANK], BF16, tag="grouped", bufs=GROUPED_BUFS, align_bytes=64)
                 regroup(nc, grouped[:], h_lin[:, g2, :, edges], BANK)
                 quantise(nc, grouped[:], h_codes[:, g2, edges], h_scales[:, g2, edges])
 
-        w2_s_chunks = load_w2_block(BLK_S)
-        rbf_s = keep.tile([P, ET, F], BF16)
-        load_rbf_block(BLK_S, rbf_s)
-        quantise_w2_block(BLK_S, w2_s_chunks, 0)
-        w2_v1_chunks = load_w2_block(BLK_V1)
-        rbf_v1 = overlay.tile([P, ET, F], BF16, offset=49152)
-        load_rbf_block(BLK_V1, rbf_v1)
-        v_sb = overlay.tile([P, ET, XD, F], BF16, offset=0)
-        v_view = v.rearrange("(p t) c j -> p t c j", t=ET)
-        for a in range(0, ET, 2):
-            nc.sync.dma_start(out=v_sb[:, a : a + 2], in_=v_view[:, a : a + 2])
-        quantise_w2_block(BLK_V1, w2_v1_chunks, 0)
+        r32 = keep.tile([P, ET, XD], F32)
+        nc.gpsimd.tensor_copy(out=r32[:], in_=r_bf[:])
+        r_sq = keep.tile([P, ET, XD], F32)
+        nc.gpsimd.tensor_tensor(out=r_sq[:], in0=r32[:], in1=r32[:], op=ALU.mult)
+        d_sq = keep.tile([P, ET], F32)
+        nc.gpsimd.tensor_tensor(out=d_sq[:], in0=r_sq[:, :, 0], in1=r_sq[:, :, 1], op=ALU.add)
+        nc.gpsimd.tensor_tensor(out=d_sq[:], in0=d_sq[:], in1=r_sq[:, :, 2], op=ALU.add)
+        dist = keep.tile([P, ET], F32)
+        nc.scalar.activation(out=dist[:], in_=d_sq[:], func=ACT.Sqrt)
+        inv_d = keep.tile([P, ET], F32)
+        nc.vector.reciprocal(out=inv_d[:], in_=dist[:])
+        d_clip = keep.tile([P, ET], F32)
+        nc.gpsimd.tensor_scalar_min(out=d_clip[:], in0=dist[:], scalar1=RC)
+        sin_d = keep.tile([P, ET], F32)
+        nc.scalar.activation(out=sin_d[:], in_=d_clip[:], func=ACT.Sin, scale=math.pi / (2.0 * RC))
+        silu_warm = keep.tile([P, 1], F32)
+        nc.scalar.activation(out=silu_warm[:], in_=sin_d[:, 0:1], func=ACT.Silu)
+        inside = keep.tile([P, ET], F32)
+        nc.gpsimd.tensor_single_scalar(out=inside[:], in_=dist[:], scalar=RC, op=ALU.is_lt)
+        sin_sq = keep.tile([P, ET], F32)
+        nc.gpsimd.tensor_tensor(out=sin_sq[:], in0=sin_d[:], in1=sin_d[:], op=ALU.mult)
+        cos_sq = keep.tile([P, ET], F32)
+        nc.gpsimd.tensor_scalar(out=cos_sq[:], in0=sin_sq[:], scalar1=-1.0, scalar2=1.0, op0=ALU.mult, op1=ALU.add)
+        fcut = keep.tile([P, ET], F32)
+        nc.gpsimd.tensor_tensor(out=fcut[:], in0=cos_sq[:], in1=inside[:], op=ALU.mult)
+        fcut_over_d = keep.tile([P, ET], F32)
+        nc.gpsimd.tensor_tensor(out=fcut_over_d[:], in0=fcut[:], in1=inv_d[:], op=ALU.mult)
+        edge_w = keep.tile([P, ET, P], F32)
+        nc.gpsimd.memset(edge_w[:], 0.0)
+        weights = keep.tile([P, ET, XD], F32)
+        nc.gpsimd.tensor_tensor(
+            out=weights[:], in0=r32[:], in1=fcut_over_d[:].unsqueeze(2).to_broadcast([P, ET, XD]), op=ALU.mult,
+        )
+        nc.gpsimd.tensor_copy(out=edge_w[:, :, 0:XD], in_=weights[:])
+        weight_sum = keep.tile([P, XD], F32)
+        nc.vector.tensor_reduce(out=weight_sum[:], in_=weights[:].rearrange("p t c -> p c t"), axis=AXIS_X, op=ALU.add)
+        w_parts = keep.tile([P, ET, PARTS, XD], BF16)
+        w_sum_parts = keep.tile([P, PARTS, XD], BF16)
+        split(nc, keep, "w", weights[:], [w_parts[:, :, i, :] for i in range(PARTS)], [P, ET, XD])
+        split(nc, keep, "ws", weight_sum[:], [w_sum_parts[:, i, :] for i in range(PARTS)], [P, XD])
 
+        quantise_s_half(0)
+        for g in range(PASSES):
+            quantise_weights(w1_raw[g], w1_codes[:, g, :], w1_scales[:, g, :], VECTOR_SHARE)
+        bias_ps = psum.tile([P, P], BF16, tag="tr", bufs=TR_BUFS)
+        nc.tensor.transpose(bias_ps[:], bias_rows[:], ident_bf[:])
+        bias_cols = keep.tile([P, P], F32)
+        nc.vector.tensor_copy(out=bias_cols[:], in_=bias_ps[:])
+
+        first_product(0)
+        quantise_s_half(1)
+        fcut_bc = keep.tile([P, E], F32)
+        for eh in range(HALVES):
+            rep_ps = psum.tile([P, BANK], F32, tag="tr", bufs=TR_BUFS)
+            for i in range(EH):
+                nc.tensor.transpose(
+                    rep_ps[:, i * P : (i + 1) * P], fcut[:, eh * EH + i : eh * EH + i + 1].to_broadcast([P, P]), ident_f[:]
+                )
+            nc.scalar.copy(out=fcut_bc[:, eh * BANK : (eh + 1) * BANK], in_=rep_ps[:])
+        quantise_w2_block(BLK_V2, w2_v2_chunks, VECTOR_SHARE)
+        first_product(1)
+
+        w2_s_chunks = load_w2_block(BLK_S)
+        rbf_s = load_rbf_block(BLK_S)
+        w2_v1_chunks = load_w2_block(BLK_V1)
+        v_view = v.rearrange("(p t) c j -> p t c j", t=ET)
+        v_sb = []
+        for a in range(0, ET, 2):
+            v_pair = overlay.tile([P, 2, XD, F], BF16, offset=(a // 2) * 12288, name="v_pair%d" % a)
+            nc.sync.dma_start(out=v_pair[:], in_=v_view[:, a : a + 2])
+            v_sb.append(v_pair)
+        rbf_v1 = load_rbf_block(BLK_V1)
+
+        filt_sum = keep.tile([P, JT, XD], F32)
         v2_acc = []
         for jh in range(F // BANK):
-            acc = psum.tile([P, BANK], F32, tag="tr", bufs=5, name="v2_acc%d" % jh)
+            acc = psum.tile([P, BANK], F32, tag="acc", bufs=2, name="v2_acc%d" % jh)
             v2_acc.append(acc)
-        for t in range(ET):
-            filt = stage.tile([P, F], F32, tag="filt", bufs=4)
-            nc.gpsimd.tensor_tensor(out=filt[:], in0=rbf_v2[:, t, :], in1=br_bc[:], op=ALU.add)
+
+        def sum_filter():
+            filt_ps = psum.tile([P, JT, PARTS, XD], F32, tag="tr", bufs=TR_BUFS)
+            for jt in range(JT):
+                cols = slice(jt * P, (jt + 1) * P)
+                for t in range(ET):
+                    nc.tensor.matmul(
+                        out=filt_ps[:, jt], lhsT=rbf_v2[t // EH][:, t % EH, cols], rhs=w_parts[:, t], start=(t == 0), stop=False
+                    )
+                nc.tensor.matmul(out=filt_ps[:, jt], lhsT=br_bc[:, cols], rhs=w_sum_parts[:], start=False, stop=True)
+            nc.vector.tensor_reduce(
+                out=filt_sum[:], in_=filt_ps[:].rearrange("p j i c -> p j c i"), axis=AXIS_X, op=ALU.add,
+            )
+
+        def edge_gate(t):
+            filt = stage.tile([P, F], F32, tag="work", bufs=WORK_BUFS, name="edge_filt")
+            nc.gpsimd.tensor_tensor(out=filt[:], in0=rbf_v2[t // EH][:, t % EH, :], in1=br_bc[:], op=ALU.add)
+            gate = stage.tile([P, F], F32, tag="work", bufs=WORK_BUFS, name="edge_gate")
             for jh in range(F // BANK):
                 cols = slice(jh * BANK, (jh + 1) * BANK)
-                phi_ps = psum.tile([P, BANK], F32, tag="phi", bufs=3)
+                phi_ps = psum.tile([P, BANK], F32, tag="phi", bufs=PHI_BUFS)
                 mx_product(
                     nc, phi_ps[:], h_codes, h_scales, slice(t * P, (t + 1) * P),
                     w2_codes, w2_scales, slice(BLK_V2 * F + jh * BANK, BLK_V2 * F + (jh + 1) * BANK),
                 )
-                phi_b = stage.tile([P, BANK], F32, tag="phi_b")
-                nc.vector.tensor_tensor(out=phi_b[:], in0=phi_ps[:], in1=b2_bc[:, cols], op=ALU.add)
-                gate = stage.tile([P, BANK], F32, tag="gate", bufs=3)
-                nc.vector.tensor_tensor(out=gate[:], in0=phi_b[:], in1=filt[:, cols], op=ALU.mult)
-                nc.tensor.matmul(out=v2_acc[jh][:], lhsT=edge_w[:, t, :], rhs=gate[:], start=(t == 0), stop=(t == ET - 1))
-        v2_rows = stage.tile([P, F], F32, tag="scratch", bufs=1)
-        res_v2 = keep.tile([P, XD, JT], F32)
-        for jh in range(F // BANK):
-            nc.vector.tensor_copy(out=v2_rows[:, jh * BANK : (jh + 1) * BANK], in_=v2_acc[jh][:])
-        for jh in range(F // BANK):
-            turn_ps = psum.tile([P, BANK // P, P], F32, tag="tr", bufs=5)
-            for i in range(BANK // P):
-                j0 = jh * BANK + i * P
-                nc.tensor.transpose(turn_ps[:, i, :], v2_rows[:, j0 : j0 + P], ident_f[:])
-            nc.vector.tensor_copy(
-                out=res_v2[:, :, jh * (BANK // P) : (jh + 1) * (BANK // P)],
-                in_=turn_ps[:, :, 0:XD].rearrange("p i c -> p c i"),
-            )
+                nc.vector.tensor_tensor(out=gate[:, cols], in0=phi_ps[:], in1=filt[:, cols], op=ALU.mult)
+            return gate
 
-        def filter_tile(blk, jt, rbf_tile):
-            rbf_ps = psum.tile([P, E], BF16, tag="tr", bufs=5)
+        def sum_gate(t, gate):
+            for jh in range(F // BANK):
+                nc.tensor.matmul(
+                    out=v2_acc[jh][:], lhsT=edge_w[:, t, :], rhs=gate[:, jh * BANK : (jh + 1) * BANK],
+                    start=(t == 0), stop=(t == ET - 1),
+                )
+
+        def turned_rbf(jt, rbf):
+            rbf_ps = psum.tile([P, E], BF16, tag="tr", bufs=TR_BUFS)
             for t in range(ET):
-                nc.tensor.transpose(rbf_ps[:, t * P : (t + 1) * P], rbf_tile[:, t, jt * P : (jt + 1) * P], ident_bf[:])
-            filt = stage.tile([P, E], F32, tag="filt", bufs=4)
-            col = ROW_BR + blk * JT + jt
+                nc.tensor.transpose(rbf_ps[:, t * P : (t + 1) * P], rbf[t // EH][:, t % EH, jt * P : (jt + 1) * P], ident_bf[:])
+            return rbf_ps
+
+        def filter_s(jt):
+            rbf_ps = turned_rbf(jt, rbf_s)
+            filt = stage.tile([P, E], F32, tag="work", bufs=WORK_BUFS, name="filt_s")
+            col = ROW_BR + BLK_S * JT + jt
             nc.scalar.activation(out=filt[:], in_=rbf_ps[:], func=ACT.Identity, bias=bias_cols[:, col : col + 1], scale=1.0)
             nc.gpsimd.tensor_tensor(out=filt[:], in0=filt[:], in1=fcut_bc[:], op=ALU.mult)
             return filt
 
+        def filter_v1(jt):
+            rbf_ps = turned_rbf(jt, rbf_v1)
+            filt = stage.tile([P, E], F32, tag="work", bufs=WORK_BUFS, name="filt_v1")
+            col = ROW_BR + BLK_V1 * JT + jt
+            nc.vector.scalar_tensor_tensor(
+                out=filt[:], in0=rbf_ps[:], scalar=bias_cols[:, col : col + 1], in1=fcut_bc[:], op0=ALU.add, op1=ALU.mult,
+            )
+            return filt
+
         def phi_tile(blk, jt, eh):
-            phi_ps = psum.tile([P, BANK], F32, tag="phi", bufs=3)
+            phi_ps = psum.tile([P, BANK], F32, tag="phi", bufs=PHI_BUFS)
             j0 = blk * F + jt * P
             mx_product(
                 nc, phi_ps[:], w2_codes, w2_scales, slice(j0, j0 + P),
@@ -290,43 +358,110 @@ def tile_message_pa_kernel(tc, s, r, v, rbf_proj, W1, b1, W2, b2, br, out_0, out
 
         res_s = keep.tile([P, JT, HALVES], F32)
         res_v1 = keep.tile([P, XD, JT], F32)
-        next_filters = (filter_tile(BLK_S, 0, rbf_s), filter_tile(BLK_V1, 0, rbf_v1))
-        for jt in range(JT):
-            filt_s, filt_v1 = next_filters
-            if jt + 1 < JT:
-                next_filters = (filter_tile(BLK_S, jt + 1, rbf_s), filter_tile(BLK_V1, jt + 1, rbf_v1))
+
+        def scalar_message(jt, filt):
             col = ROW_B2 + BLK_S * JT + jt
             for eh in range(HALVES):
                 phi_ps = phi_tile(BLK_S, jt, eh)
                 nc.vector.scalar_tensor_tensor(
-                    out=filt_s[:, eh * BANK : (eh + 1) * BANK], in0=phi_ps[:], scalar=bias_cols[:, col : col + 1],
-                    in1=filt_s[:, eh * BANK : (eh + 1) * BANK], op0=ALU.add, op1=ALU.mult,
+                    out=filt[:, eh * BANK : (eh + 1) * BANK], in0=phi_ps[:], scalar=bias_cols[:, col : col + 1],
+                    in1=filt[:, eh * BANK : (eh + 1) * BANK], op0=ALU.add, op1=ALU.mult,
                     accum_out=res_s[:, jt, eh : eh + 1],
                 )
+
+        def vector_gate(jt, filt):
             col = ROW_B2 + BLK_V1 * JT + jt
-            gate = stage.tile([P, E], F32, tag="gate_t")
+            gate = stage.tile([P, E], F32, tag="work", bufs=WORK_BUFS, name="vector_gate")
             for eh in range(HALVES):
+                edges = slice(eh * BANK, (eh + 1) * BANK)
                 phi_ps = phi_tile(BLK_V1, jt, eh)
                 nc.vector.scalar_tensor_tensor(
-                    out=gate[:, eh * BANK : (eh + 1) * BANK], in0=phi_ps[:], scalar=bias_cols[:, col : col + 1],
-                    in1=filt_v1[:, eh * BANK : (eh + 1) * BANK], op0=ALU.add, op1=ALU.mult,
+                    out=gate[:, edges], in0=phi_ps[:], scalar=bias_cols[:, col : col + 1],
+                    in1=filt[:, edges], op0=ALU.add, op1=ALU.mult,
                 )
-            for c in range(XD):
-                v_ps = psum.tile([P, E], BF16, tag="tr", bufs=5)
-                for t in range(ET):
-                    nc.tensor.transpose(v_ps[:, t * P : (t + 1) * P], v_sb[:, t, c, jt * P : (jt + 1) * P], ident_bf[:])
-                nc.vector.scalar_tensor_tensor(
-                    out=filt_v1[:], in0=v_ps[:], scalar=1.0, in1=gate[:], op0=ALU.mult, op1=ALU.mult,
-                    accum_out=res_v1[:, c, jt : jt + 1],
-                )
+            return gate
 
-        res = keep.tile([P, P], F32)
-        nc.vector.memset(res[:], 0.0)
+        def vector_message(jt, gate, spent):
+            for c in reversed(range(XD)):
+                on_gpsimd = c == XD - 1 and jt < GPSIMD_TILES
+                if on_gpsimd:
+                    v_ps = psum.tile([P, E], BF16, tag="acc", bufs=2, name="v_ps_gpsimd")
+                else:
+                    v_ps = psum.tile([P, E], BF16, tag="tr", bufs=TR_BUFS)
+                for t in range(ET):
+                    nc.tensor.transpose(v_ps[:, t * P : (t + 1) * P], v_sb[t // 2][:, t % 2, c, jt * P : (jt + 1) * P], ident_bf[:])
+                if on_gpsimd:
+                    product = stage.tile([P, E], F32, tag="work", bufs=WORK_BUFS, name="product")
+                    v_copy = stage.tile([P, E], BF16, tag="work", bufs=WORK_BUFS, name="v_copy")
+                    nc.scalar.copy(out=v_copy[:], in_=v_ps[:])
+                    nc.gpsimd.tensor_tensor(out=product[:], in0=gate[:], in1=v_copy[:], op=ALU.mult)
+                    products[jt] = product
+                else:
+                    nc.vector.scalar_tensor_tensor(
+                        out=spent[:], in0=v_ps[:], scalar=1.0, in1=gate[:], op0=ALU.mult, op1=ALU.mult,
+                        accum_out=res_v1[:, c, jt : jt + 1],
+                    )
+
+        products = {}
+
+        def sum_product(jt):
+            nc.scalar.activation(
+                out=products[jt][:], in_=products[jt][:], func=ACT.Identity, accum_out=res_v1[:, XD - 1, jt : jt + 1],
+            )
+
+        sum_filter()
+        edge_gates = {}
+        filters_s = {}
+        filters_v1 = {}
+        for i in range(JT + LAG_V1):
+            if i < ET:
+                edge_gates[i] = edge_gate(i)
+            if i == 1:
+                quantise_w2_block(BLK_S, w2_s_chunks, VECTOR_SHARE)
+            if i == 3:
+                quantise_w2_block(BLK_V1, w2_v1_chunks, 0)
+            if 0 <= i - LAG_S + 1 < JT:
+                filters_s[i - LAG_S + 1] = filter_s(i - LAG_S + 1)
+            if 0 <= i - LAG_S < JT:
+                scalar_message(i - LAG_S, filters_s[i - LAG_S])
+            if 0 <= i - 1 < ET:
+                sum_gate(i - 1, edge_gates[i - 1])
+            if 0 <= i - LAG_V1:
+                filters_v1[i - LAG_V1] = filter_v1(i - LAG_V1)
+        v2_rows = stage.tile([P, F], F32, tag="work", bufs=WORK_BUFS)
+        gate_sum = keep.tile([P, JT, XD], F32)
+        for jh in range(F // BANK):
+            nc.scalar.copy(out=v2_rows[:, jh * BANK : (jh + 1) * BANK], in_=v2_acc[jh][:])
+        for jh in range(F // BANK):
+            turn_ps = psum.tile([P, BANK // P, P], F32, tag="acc", bufs=2)
+            for i in range(BANK // P):
+                j0 = jh * BANK + i * P
+                nc.tensor.transpose(turn_ps[:, i, :], v2_rows[:, j0 : j0 + P], ident_f[:])
+            nc.vector.tensor_copy(
+                out=gate_sum[:, jh * (BANK // P) : (jh + 1) * (BANK // P), :], in_=turn_ps[:, :, 0:XD],
+            )
+        gate = vector_gate(0, filters_v1[0])
+        for jt in range(JT):
+            next_gate = vector_gate(jt + 1, filters_v1[jt + 1]) if jt + 1 < JT else None
+            vector_message(jt, gate, filters_v1[jt])
+            if jt - 1 in products:
+                sum_product(jt - 1)
+            gate = next_gate
+
+        b2_cols = bias_cols[:, ROW_B2 + BLK_V2 * JT : ROW_B2 + (BLK_V2 + 1) * JT]
+        res_v2 = keep.tile([P, JT, XD], F32)
         nc.vector.tensor_tensor(
-            out=res[:, 0 : XD * JT].rearrange("p (c j) -> p c j", c=XD), in0=res_v1[:], in1=res_v2[:], op=ALU.add,
+            out=res_v2[:], in0=filt_sum[:], in1=b2_cols.unsqueeze(2).to_broadcast([P, JT, XD]), op=ALU.mult,
         )
+        nc.vector.tensor_tensor(out=res_v2[:], in0=res_v2[:], in1=gate_sum[:], op=ALU.add)
+        res = keep.tile([P, P], F32)
+        nc.gpsimd.memset(res[:], 0.0)
         nc.vector.tensor_tensor(out=res[:, XD * JT : (XD + 1) * JT], in0=res_s[:, :, 0], in1=res_s[:, :, 1], op=ALU.add)
-        res_ps = psum.tile([P, P], F32, tag="tr", bufs=5)
+        nc.vector.tensor_tensor(
+            out=res[:, 0 : XD * JT].rearrange("p (c j) -> p c j", c=XD), in0=res_v1[:],
+            in1=res_v2[:].rearrange("p j c -> p c j"), op=ALU.add,
+        )
+        res_ps = psum.tile([P, P], F32, tag="tr", bufs=TR_BUFS)
         nc.tensor.transpose(res_ps[:], res[:], ident_f[:])
         res_rows = keep.tile([P, P], F32)
         nc.vector.tensor_copy(out=res_rows[:], in_=res_ps[:])

@@ -29,15 +29,14 @@ BLK_V1, BLK_S, BLK_V2 = 0, 1, 2
 ROW_B2, ROW_BR, ROW_B1 = 0, 32, 64
 PARTS = 3
 VECTOR_SHARE = 344
-GPSIMD_TILES = 6
+GPSIMD_TILES = range(1, 7)
 RAW_BUFS = 3
-GROUPED_BUFS = 5
+GROUPED_BUFS = 4
 RBF_BUFS = 5
-WORK_BUFS = 10
+WORK_BUFS = 12
+AHEAD = 2
 TR_BUFS = 3
 PHI_BUFS = 3
-LAG_S = 2
-LAG_V1 = 5
 
 FLOPS = 2 * E * F * F + 2 * E * F * 3 * F
 
@@ -154,10 +153,12 @@ def tile_message_pa_kernel(tc, s, r, v, rbf_proj, W1, b1, W2, b2, br, out_0, out
         w2_codes = keep.tile([P, PASSES, 3 * F], U32, align_bytes=64)
         w2_scales = keep.tile([P, PASSES, 3 * F], U8, align_bytes=64)
 
-        w2_v2_chunks = load_w2_block(BLK_V2)
+        w2_s_chunks = load_w2_block(BLK_S)
+        rbf_s = load_rbf_block(BLK_S)
+        w2_v1_chunks = load_w2_block(BLK_V1)
+        rbf_v1 = load_rbf_block(BLK_V1)
         br_bc = keep.tile([P, F], BF16)
         nc.sync.dma_start(out=br_bc[:], in_=br[BLK_V2 * F : (BLK_V2 + 1) * F].partition_broadcast(P))
-        rbf_v2 = load_rbf_block(BLK_V2)
 
         def quantise_weights(raw, codes, scales, vector_cols):
             for c0 in range(0, F, BANK):
@@ -270,19 +271,18 @@ def tile_message_pa_kernel(tc, s, r, v, rbf_proj, W1, b1, W2, b2, br, out_0, out
                     rep_ps[:, i * P : (i + 1) * P], fcut[:, eh * EH + i : eh * EH + i + 1].to_broadcast([P, P]), ident_f[:]
                 )
             nc.scalar.copy(out=fcut_bc[:, eh * BANK : (eh + 1) * BANK], in_=rep_ps[:])
-        quantise_w2_block(BLK_V2, w2_v2_chunks, VECTOR_SHARE)
+        quantise_w2_block(BLK_S, w2_s_chunks, VECTOR_SHARE)
         first_product(1)
+        quantise_w2_block(BLK_V1, w2_v1_chunks, VECTOR_SHARE)
 
-        w2_s_chunks = load_w2_block(BLK_S)
-        rbf_s = load_rbf_block(BLK_S)
-        w2_v1_chunks = load_w2_block(BLK_V1)
         v_view = v.rearrange("(p t) c j -> p t c j", t=ET)
         v_sb = []
         for a in range(0, ET, 2):
             v_pair = overlay.tile([P, 2, XD, F], BF16, offset=(a // 2) * 12288, name="v_pair%d" % a)
             nc.sync.dma_start(out=v_pair[:], in_=v_view[:, a : a + 2])
             v_sb.append(v_pair)
-        rbf_v1 = load_rbf_block(BLK_V1)
+        w2_v2_chunks = load_w2_block(BLK_V2)
+        rbf_v2 = load_rbf_block(BLK_V2)
 
         filt_sum = keep.tile([P, JT, XD], F32)
         v2_acc = []
@@ -303,26 +303,26 @@ def tile_message_pa_kernel(tc, s, r, v, rbf_proj, W1, b1, W2, b2, br, out_0, out
                 out=filt_sum[:], in_=filt_ps[:].rearrange("p j i c -> p j c i"), axis=AXIS_X, op=ALU.add,
             )
 
-        def edge_gate(t):
+        def edge_filter(t):
             filt = stage.tile([P, F], F32, tag="work", bufs=WORK_BUFS, name="edge_filt")
             nc.gpsimd.tensor_tensor(out=filt[:], in0=rbf_v2[t // EH][:, t % EH, :], in1=br_bc[:], op=ALU.add)
             gate = stage.tile([P, F], F32, tag="work", bufs=WORK_BUFS, name="edge_gate")
-            for jh in range(F // BANK):
-                cols = slice(jh * BANK, (jh + 1) * BANK)
-                phi_ps = psum.tile([P, BANK], F32, tag="phi", bufs=PHI_BUFS)
-                mx_product(
-                    nc, phi_ps[:], h_codes, h_scales, slice(t * P, (t + 1) * P),
-                    w2_codes, w2_scales, slice(BLK_V2 * F + jh * BANK, BLK_V2 * F + (jh + 1) * BANK),
-                )
-                nc.vector.tensor_tensor(out=gate[:, cols], in0=phi_ps[:], in1=filt[:, cols], op=ALU.mult)
-            return gate
+            return filt, gate
 
-        def sum_gate(t, gate):
-            for jh in range(F // BANK):
-                nc.tensor.matmul(
-                    out=v2_acc[jh][:], lhsT=edge_w[:, t, :], rhs=gate[:, jh * BANK : (jh + 1) * BANK],
-                    start=(t == 0), stop=(t == ET - 1),
-                )
+        def edge_gate(t, jh, filt, gate):
+            cols = slice(jh * BANK, (jh + 1) * BANK)
+            phi_ps = psum.tile([P, BANK], F32, tag="phi", bufs=PHI_BUFS)
+            mx_product(
+                nc, phi_ps[:], h_codes, h_scales, slice(t * P, (t + 1) * P),
+                w2_codes, w2_scales, slice(BLK_V2 * F + jh * BANK, BLK_V2 * F + (jh + 1) * BANK),
+            )
+            nc.vector.tensor_tensor(out=gate[:, cols], in0=phi_ps[:], in1=filt[:, cols], op=ALU.mult)
+
+        def sum_gate(t, jh, gate):
+            nc.tensor.matmul(
+                out=v2_acc[jh][:], lhsT=edge_w[:, t, :], rhs=gate[:, jh * BANK : (jh + 1) * BANK],
+                start=(t == 0), stop=(t == ET - 1),
+            )
 
         def turned_rbf(jt, rbf):
             rbf_ps = psum.tile([P, E], BF16, tag="tr", bufs=TR_BUFS)
@@ -381,26 +381,22 @@ def tile_message_pa_kernel(tc, s, r, v, rbf_proj, W1, b1, W2, b2, br, out_0, out
                 )
             return gate
 
-        def vector_message(jt, gate, spent):
-            for c in reversed(range(XD)):
-                on_gpsimd = c == XD - 1 and jt < GPSIMD_TILES
-                if on_gpsimd:
-                    v_ps = psum.tile([P, E], BF16, tag="acc", bufs=2, name="v_ps_gpsimd")
-                else:
-                    v_ps = psum.tile([P, E], BF16, tag="tr", bufs=TR_BUFS)
-                for t in range(ET):
-                    nc.tensor.transpose(v_ps[:, t * P : (t + 1) * P], v_sb[t // 2][:, t % 2, c, jt * P : (jt + 1) * P], ident_bf[:])
-                if on_gpsimd:
-                    product = stage.tile([P, E], F32, tag="work", bufs=WORK_BUFS, name="product")
-                    v_copy = stage.tile([P, E], BF16, tag="work", bufs=WORK_BUFS, name="v_copy")
-                    nc.scalar.copy(out=v_copy[:], in_=v_ps[:])
-                    nc.gpsimd.tensor_tensor(out=product[:], in0=gate[:], in1=v_copy[:], op=ALU.mult)
-                    products[jt] = product
-                else:
-                    nc.vector.scalar_tensor_tensor(
-                        out=spent[:], in0=v_ps[:], scalar=1.0, in1=gate[:], op0=ALU.mult, op1=ALU.mult,
-                        accum_out=res_v1[:, c, jt : jt + 1],
-                    )
+        def vector_message(jt, c, gate, spent):
+            on_gpsimd = c == XD - 1 and jt in GPSIMD_TILES
+            v_ps = psum.tile([P, E], BF16, tag="tr", bufs=TR_BUFS)
+            for t in range(ET):
+                nc.tensor.transpose(v_ps[:, t * P : (t + 1) * P], v_sb[t // 2][:, t % 2, c, jt * P : (jt + 1) * P], ident_bf[:])
+            if on_gpsimd:
+                product = stage.tile([P, E], F32, tag="work", bufs=WORK_BUFS, name="product")
+                v_copy = stage.tile([P, E], BF16, tag="work", bufs=WORK_BUFS, name="v_copy")
+                nc.scalar.copy(out=v_copy[:], in_=v_ps[:])
+                nc.gpsimd.tensor_tensor(out=product[:], in0=gate[:], in1=v_copy[:], op=ALU.mult)
+                products[jt] = product
+            else:
+                nc.vector.scalar_tensor_tensor(
+                    out=spent[:], in0=v_ps[:], scalar=1.0, in1=gate[:], op0=ALU.mult, op1=ALU.mult,
+                    accum_out=res_v1[:, c, jt : jt + 1],
+                )
 
         products = {}
 
@@ -409,44 +405,48 @@ def tile_message_pa_kernel(tc, s, r, v, rbf_proj, W1, b1, W2, b2, br, out_0, out
                 out=products[jt][:], in_=products[jt][:], func=ACT.Identity, accum_out=res_v1[:, XD - 1, jt : jt + 1],
             )
 
+        gates_v1 = []
+        filters_s = [filter_s(jt) for jt in range(AHEAD)]
+        filt_v1 = filter_v1(0)
+        for jt in range(JT):
+            if jt + AHEAD < JT:
+                filters_s.append(filter_s(jt + AHEAD))
+            scalar_message(jt, filters_s[jt])
+            next_v1 = filter_v1(jt + 1) if jt + 1 < JT else None
+            gates_v1.append(vector_gate(jt, filt_v1))
+            filt_v1 = next_v1
+            if jt == JT // 2:
+                quantise_w2_block(BLK_V2, w2_v2_chunks, 0)
+
         sum_filter()
-        edge_gates = {}
-        filters_s = {}
-        filters_v1 = {}
-        for i in range(JT + LAG_V1):
-            if i < ET:
-                edge_gates[i] = edge_gate(i)
-            if i == 1:
-                quantise_w2_block(BLK_S, w2_s_chunks, VECTOR_SHARE)
-            if i == 3:
-                quantise_w2_block(BLK_V1, w2_v1_chunks, 0)
-            if 0 <= i - LAG_S + 1 < JT:
-                filters_s[i - LAG_S + 1] = filter_s(i - LAG_S + 1)
-            if 0 <= i - LAG_S < JT:
-                scalar_message(i - LAG_S, filters_s[i - LAG_S])
-            if 0 <= i - 1 < ET:
-                sum_gate(i - 1, edge_gates[i - 1])
-            if 0 <= i - LAG_V1:
-                filters_v1[i - LAG_V1] = filter_v1(i - LAG_V1)
-        v2_rows = stage.tile([P, F], F32, tag="work", bufs=WORK_BUFS)
+        spent, gate = edge_filter(0)
+        for jh in range(F // BANK):
+            edge_gate(0, jh, spent, gate)
+        for i in range(ET):
+            if i + 1 < ET:
+                next_edge = edge_filter(i + 1)
+            for c in reversed(range(XD)):
+                vector_message(i, c, gates_v1[i], spent)
+                if c > 0:
+                    jh = XD - 1 - c
+                    if i + 1 < ET:
+                        edge_gate(i + 1, jh, *next_edge)
+                    sum_gate(i, jh, gate)
+            if i - 1 in products:
+                sum_product(i - 1)
+            spent, gate = next_edge
         gate_sum = keep.tile([P, JT, XD], F32)
+        v2_rows = stage.tile([P, F], F32, tag="work", bufs=WORK_BUFS)
         for jh in range(F // BANK):
             nc.scalar.copy(out=v2_rows[:, jh * BANK : (jh + 1) * BANK], in_=v2_acc[jh][:])
         for jh in range(F // BANK):
             turn_ps = psum.tile([P, BANK // P, P], F32, tag="acc", bufs=2)
-            for i in range(BANK // P):
-                j0 = jh * BANK + i * P
-                nc.tensor.transpose(turn_ps[:, i, :], v2_rows[:, j0 : j0 + P], ident_f[:])
+            for k in range(BANK // P):
+                j0 = jh * BANK + k * P
+                nc.tensor.transpose(turn_ps[:, k, :], v2_rows[:, j0 : j0 + P], ident_f[:])
             nc.vector.tensor_copy(
                 out=gate_sum[:, jh * (BANK // P) : (jh + 1) * (BANK // P), :], in_=turn_ps[:, :, 0:XD],
             )
-        gate = vector_gate(0, filters_v1[0])
-        for jt in range(JT):
-            next_gate = vector_gate(jt + 1, filters_v1[jt + 1]) if jt + 1 < JT else None
-            vector_message(jt, gate, filters_v1[jt])
-            if jt - 1 in products:
-                sum_product(jt - 1)
-            gate = next_gate
 
         b2_cols = bias_cols[:, ROW_B2 + BLK_V2 * JT : ROW_B2 + (BLK_V2 + 1) * JT]
         res_v2 = keep.tile([P, JT, XD], F32)

@@ -35,6 +35,7 @@ GROUPED_BUFS = 4
 RBF_BUFS = 5
 WORK_BUFS = 12
 AHEAD = 2
+LAG_V1 = 2
 TR_BUFS = 3
 PHI_BUFS = 3
 
@@ -160,16 +161,16 @@ def tile_message_pa_kernel(tc, s, r, v, rbf_proj, W1, b1, W2, b2, br, out_0, out
         br_bc = keep.tile([P, F], BF16)
         nc.sync.dma_start(out=br_bc[:], in_=br[BLK_V2 * F : (BLK_V2 + 1) * F].partition_broadcast(P))
 
-        def quantise_weights(raw, codes, scales, vector_cols):
+        def quantise_weights(chunks, codes, scales, col0, vector_cols):
             for c0 in range(0, F, BANK):
-                grouped = stage.tile([P, PACK * BANK], BF16, tag="grouped", bufs=GROUPED_BUFS, align_bytes=64)
-                regroup(nc, grouped[:], raw[:, :, c0 : c0 + BANK], vector_cols)
-                quantise(nc, grouped[:], codes[:, c0 : c0 + BANK], scales[:, c0 : c0 + BANK])
+                for g in range(PASSES):
+                    grouped = stage.tile([P, PACK * BANK], BF16, tag="grouped", bufs=GROUPED_BUFS, align_bytes=64)
+                    regroup(nc, grouped[:], chunks[g][:, :, c0 : c0 + BANK], vector_cols)
+                    cols = slice(col0 + c0, col0 + c0 + BANK)
+                    quantise(nc, grouped[:], codes[:, g, cols], scales[:, g, cols])
 
         def quantise_w2_block(blk, chunks, vector_cols):
-            cols = slice(blk * F, (blk + 1) * F)
-            for g in range(PASSES):
-                quantise_weights(chunks[g], w2_codes[:, g, cols], w2_scales[:, g, cols], vector_cols)
+            quantise_weights(chunks, w2_codes, w2_scales, blk * F, vector_cols)
 
         s_words = s_raw[:].bitcast(F32)
 
@@ -189,7 +190,7 @@ def tile_message_pa_kernel(tc, s, r, v, rbf_proj, W1, b1, W2, b2, br, out_0, out
                             )
                     dst = grouped[g][:].bitcast(F32).rearrange("p (e u) -> p e u", u=2)
                     dst = dst[:, tp * 2 * P : (tp + 1) * 2 * P, :]
-                    if g == 0:
+                    if g == 0 and eh == 0:
                         nc.vector.tensor_copy(out=dst, in_=s_ps[:].rearrange("p u e -> p e u"))
                     else:
                         nc.scalar.copy(out=dst, in_=s_ps[:].rearrange("p u e -> p e u"))
@@ -254,15 +255,14 @@ def tile_message_pa_kernel(tc, s, r, v, rbf_proj, W1, b1, W2, b2, br, out_0, out
         split(nc, keep, "ws", weight_sum[:], [w_sum_parts[:, i, :] for i in range(PARTS)], [P, XD])
 
         quantise_s_half(0)
-        for g in range(PASSES):
-            quantise_weights(w1_raw[g], w1_codes[:, g, :], w1_scales[:, g, :], VECTOR_SHARE)
+        quantise_weights(w1_raw, w1_codes, w1_scales, 0, VECTOR_SHARE)
         bias_ps = psum.tile([P, P], BF16, tag="tr", bufs=TR_BUFS)
         nc.tensor.transpose(bias_ps[:], bias_rows[:], ident_bf[:])
         bias_cols = keep.tile([P, P], F32)
-        nc.vector.tensor_copy(out=bias_cols[:], in_=bias_ps[:])
+        nc.scalar.copy(out=bias_cols[:], in_=bias_ps[:])
 
-        first_product(0)
         quantise_s_half(1)
+        first_product(0)
         fcut_bc = keep.tile([P, E], F32)
         for eh in range(HALVES):
             rep_ps = psum.tile([P, BANK], F32, tag="tr", bufs=TR_BUFS)
@@ -272,8 +272,32 @@ def tile_message_pa_kernel(tc, s, r, v, rbf_proj, W1, b1, W2, b2, br, out_0, out
                 )
             nc.scalar.copy(out=fcut_bc[:, eh * BANK : (eh + 1) * BANK], in_=rep_ps[:])
         quantise_w2_block(BLK_S, w2_s_chunks, VECTOR_SHARE)
+        def turned_rbf(jt, rbf):
+            rbf_ps = psum.tile([P, E], BF16, tag="tr", bufs=TR_BUFS)
+            for t in range(ET):
+                nc.tensor.transpose(rbf_ps[:, t * P : (t + 1) * P], rbf[t // EH][:, t % EH, jt * P : (jt + 1) * P], ident_bf[:])
+            return rbf_ps
+
+        def filter_s(jt):
+            rbf_ps = turned_rbf(jt, rbf_s)
+            filt = stage.tile([P, E], F32, tag="work", bufs=WORK_BUFS, name="filt_s")
+            col = ROW_BR + BLK_S * JT + jt
+            nc.scalar.activation(out=filt[:], in_=rbf_ps[:], func=ACT.Identity, bias=bias_cols[:, col : col + 1], scale=1.0)
+            nc.gpsimd.tensor_tensor(out=filt[:], in0=filt[:], in1=fcut_bc[:], op=ALU.mult)
+            return filt
+
+        def filter_v1(jt):
+            rbf_ps = turned_rbf(jt, rbf_v1)
+            filt = stage.tile([P, E], F32, tag="work", bufs=WORK_BUFS, name="filt_v1")
+            col = ROW_BR + BLK_V1 * JT + jt
+            nc.vector.scalar_tensor_tensor(
+                out=filt[:], in0=rbf_ps[:], scalar=bias_cols[:, col : col + 1], in1=fcut_bc[:], op0=ALU.add, op1=ALU.mult,
+            )
+            return filt
+
+        filters_s = [filter_s(jt) for jt in range(AHEAD)]
         first_product(1)
-        quantise_w2_block(BLK_V1, w2_v1_chunks, VECTOR_SHARE)
+        quantise_w2_block(BLK_V1, w2_v1_chunks, 0)
 
         v_view = v.rearrange("(p t) c j -> p t c j", t=ET)
         v_sb = []
@@ -324,29 +348,6 @@ def tile_message_pa_kernel(tc, s, r, v, rbf_proj, W1, b1, W2, b2, br, out_0, out
                 start=(t == 0), stop=(t == ET - 1),
             )
 
-        def turned_rbf(jt, rbf):
-            rbf_ps = psum.tile([P, E], BF16, tag="tr", bufs=TR_BUFS)
-            for t in range(ET):
-                nc.tensor.transpose(rbf_ps[:, t * P : (t + 1) * P], rbf[t // EH][:, t % EH, jt * P : (jt + 1) * P], ident_bf[:])
-            return rbf_ps
-
-        def filter_s(jt):
-            rbf_ps = turned_rbf(jt, rbf_s)
-            filt = stage.tile([P, E], F32, tag="work", bufs=WORK_BUFS, name="filt_s")
-            col = ROW_BR + BLK_S * JT + jt
-            nc.scalar.activation(out=filt[:], in_=rbf_ps[:], func=ACT.Identity, bias=bias_cols[:, col : col + 1], scale=1.0)
-            nc.gpsimd.tensor_tensor(out=filt[:], in0=filt[:], in1=fcut_bc[:], op=ALU.mult)
-            return filt
-
-        def filter_v1(jt):
-            rbf_ps = turned_rbf(jt, rbf_v1)
-            filt = stage.tile([P, E], F32, tag="work", bufs=WORK_BUFS, name="filt_v1")
-            col = ROW_BR + BLK_V1 * JT + jt
-            nc.vector.scalar_tensor_tensor(
-                out=filt[:], in0=rbf_ps[:], scalar=bias_cols[:, col : col + 1], in1=fcut_bc[:], op0=ALU.add, op1=ALU.mult,
-            )
-            return filt
-
         def phi_tile(blk, jt, eh):
             phi_ps = psum.tile([P, BANK], F32, tag="phi", bufs=PHI_BUFS)
             j0 = blk * F + jt * P
@@ -387,8 +388,8 @@ def tile_message_pa_kernel(tc, s, r, v, rbf_proj, W1, b1, W2, b2, br, out_0, out
             for t in range(ET):
                 nc.tensor.transpose(v_ps[:, t * P : (t + 1) * P], v_sb[t // 2][:, t % 2, c, jt * P : (jt + 1) * P], ident_bf[:])
             if on_gpsimd:
-                product = stage.tile([P, E], F32, tag="work", bufs=WORK_BUFS, name="product")
-                v_copy = stage.tile([P, E], BF16, tag="work", bufs=WORK_BUFS, name="v_copy")
+                product = stage.tile([P, E], F32, tag="raw", bufs=RAW_BUFS, name="product")
+                v_copy = stage.tile([P, E], BF16, tag="grouped", bufs=GROUPED_BUFS, align_bytes=64, name="v_copy")
                 nc.scalar.copy(out=v_copy[:], in_=v_ps[:])
                 nc.gpsimd.tensor_tensor(out=product[:], in0=gate[:], in1=v_copy[:], op=ALU.mult)
                 products[jt] = product
@@ -406,16 +407,18 @@ def tile_message_pa_kernel(tc, s, r, v, rbf_proj, W1, b1, W2, b2, br, out_0, out
             )
 
         gates_v1 = []
-        filters_s = [filter_s(jt) for jt in range(AHEAD)]
-        filt_v1 = filter_v1(0)
-        for jt in range(JT):
-            if jt + AHEAD < JT:
-                filters_s.append(filter_s(jt + AHEAD))
-            scalar_message(jt, filters_s[jt])
-            next_v1 = filter_v1(jt + 1) if jt + 1 < JT else None
-            gates_v1.append(vector_gate(jt, filt_v1))
-            filt_v1 = next_v1
-            if jt == JT // 2:
+        next_v1 = filter_v1(0)
+        for i in range(JT + LAG_V1):
+            if i + AHEAD < JT:
+                filters_s.append(filter_s(i + AHEAD))
+            if i < JT:
+                scalar_message(i, filters_s[i])
+            if i >= LAG_V1:
+                filt_v1 = next_v1
+                if i - LAG_V1 + 1 < JT:
+                    next_v1 = filter_v1(i - LAG_V1 + 1)
+                gates_v1.append(vector_gate(i - LAG_V1, filt_v1))
+            if i == JT // 2:
                 quantise_w2_block(BLK_V2, w2_v2_chunks, 0)
 
         sum_filter()

@@ -34,7 +34,7 @@ RAW_BUFS = 3
 GROUPED_BUFS = 4
 RBF_BUFS = 5
 WORK_BUFS = 12
-AHEAD = 2
+AHEAD = 1
 LAG_V1 = 2
 TR_BUFS = 3
 PHI_BUFS = 3
@@ -282,8 +282,9 @@ def tile_message_pa_kernel(tc, s, r, v, rbf_proj, W1, b1, W2, b2, br, out_0, out
             rbf_ps = turned_rbf(jt, rbf_s)
             filt = stage.tile([P, E], F32, tag="work", bufs=WORK_BUFS, name="filt_s")
             col = ROW_BR + BLK_S * JT + jt
-            nc.scalar.activation(out=filt[:], in_=rbf_ps[:], func=ACT.Identity, bias=bias_cols[:, col : col + 1], scale=1.0)
-            nc.gpsimd.tensor_tensor(out=filt[:], in0=filt[:], in1=fcut_bc[:], op=ALU.mult)
+            nc.vector.scalar_tensor_tensor(
+                out=filt[:], in0=rbf_ps[:], scalar=bias_cols[:, col : col + 1], in1=fcut_bc[:], op0=ALU.add, op1=ALU.mult,
+            )
             return filt
 
         def filter_v1(jt):
@@ -295,7 +296,6 @@ def tile_message_pa_kernel(tc, s, r, v, rbf_proj, W1, b1, W2, b2, br, out_0, out
             )
             return filt
 
-        filters_s = [filter_s(jt) for jt in range(AHEAD)]
         first_product(1)
         quantise_w2_block(BLK_V1, w2_v1_chunks, 0)
 
@@ -407,6 +407,7 @@ def tile_message_pa_kernel(tc, s, r, v, rbf_proj, W1, b1, W2, b2, br, out_0, out
             )
 
         gates_v1 = []
+        filters_s = [filter_s(jt) for jt in range(AHEAD)]
         next_v1 = filter_v1(0)
         for i in range(JT + LAG_V1):
             if i + AHEAD < JT:

@@ -29,11 +29,12 @@ BLK_V1, BLK_S, BLK_V2 = 0, 1, 2
 ROW_B2, ROW_BR, ROW_B1 = 0, 32, 64
 PARTS = 3
 VECTOR_SHARE = 344
-GPSIMD_TILES = range(1, 7)
+GPSIMD_TILES = range(6)
 RAW_BUFS = 3
 GROUPED_BUFS = 4
 RBF_BUFS = 5
 WORK_BUFS = 12
+GPSIMD_FILTERS_FROM = 3
 AHEAD = 1
 LAG_V1 = 2
 TR_BUFS = 3
@@ -291,24 +292,28 @@ def tile_message_pa_kernel(tc, s, r, v, rbf_proj, W1, b1, W2, b2, br, out_0, out
             rbf_ps = turned_rbf(jt, rbf_v1)
             filt = stage.tile([P, E], F32, tag="work", bufs=WORK_BUFS, name="filt_v1")
             col = ROW_BR + BLK_V1 * JT + jt
-            nc.vector.scalar_tensor_tensor(
-                out=filt[:], in0=rbf_ps[:], scalar=bias_cols[:, col : col + 1], in1=fcut_bc[:], op0=ALU.add, op1=ALU.mult,
-            )
+            if jt < GPSIMD_FILTERS_FROM:
+                nc.vector.scalar_tensor_tensor(
+                    out=filt[:], in0=rbf_ps[:], scalar=bias_cols[:, col : col + 1], in1=fcut_bc[:], op0=ALU.add, op1=ALU.mult,
+                )
+            else:
+                nc.scalar.activation(out=filt[:], in_=rbf_ps[:], func=ACT.Identity, bias=bias_cols[:, col : col + 1], scale=1.0)
+                nc.gpsimd.tensor_tensor(out=filt[:], in0=filt[:], in1=fcut_bc[:], op=ALU.mult)
             return filt
 
         first_product(1)
         quantise_w2_block(BLK_V1, w2_v1_chunks, 0)
 
+        w2_v2_chunks = load_w2_block(BLK_V2)
         v_view = v.rearrange("(p t) c j -> p t c j", t=ET)
         v_sb = []
         for a in range(0, ET, 2):
             v_pair = overlay.tile([P, 2, XD, F], BF16, offset=(a // 2) * 12288, name="v_pair%d" % a)
             nc.sync.dma_start(out=v_pair[:], in_=v_view[:, a : a + 2])
             v_sb.append(v_pair)
-        w2_v2_chunks = load_w2_block(BLK_V2)
         rbf_v2 = load_rbf_block(BLK_V2)
 
-        filt_sum = keep.tile([P, JT, XD], F32)
+        terms_v2 = keep.tile([P, JT, PARTS + 1, XD], F32)
         v2_acc = []
         for jh in range(F // BANK):
             acc = psum.tile([P, BANK], F32, tag="acc", bufs=2, name="v2_acc%d" % jh)
@@ -323,9 +328,11 @@ def tile_message_pa_kernel(tc, s, r, v, rbf_proj, W1, b1, W2, b2, br, out_0, out
                         out=filt_ps[:, jt], lhsT=rbf_v2[t // EH][:, t % EH, cols], rhs=w_parts[:, t], start=(t == 0), stop=False
                     )
                 nc.tensor.matmul(out=filt_ps[:, jt], lhsT=br_bc[:, cols], rhs=w_sum_parts[:], start=False, stop=True)
-            nc.vector.tensor_reduce(
-                out=filt_sum[:], in_=filt_ps[:].rearrange("p j i c -> p j c i"), axis=AXIS_X, op=ALU.add,
-            )
+            for jt in range(JT):
+                col = ROW_B2 + BLK_V2 * JT + jt
+                nc.scalar.activation(
+                    out=terms_v2[:, jt, 0:PARTS, :], in_=filt_ps[:, jt], func=ACT.Copy, scale=bias_cols[:, col : col + 1],
+                )
 
         def edge_filter(t):
             filt = stage.tile([P, F], F32, tag="work", bufs=WORK_BUFS, name="edge_filt")
@@ -407,57 +414,59 @@ def tile_message_pa_kernel(tc, s, r, v, rbf_proj, W1, b1, W2, b2, br, out_0, out
             )
 
         gates_v1 = []
+        edges = []
         filters_s = [filter_s(jt) for jt in range(AHEAD)]
-        next_v1 = filter_v1(0)
+        filters_v1 = [filter_v1(0), filter_v1(1)]
         for i in range(JT + LAG_V1):
             if i + AHEAD < JT:
                 filters_s.append(filter_s(i + AHEAD))
             if i < JT:
                 scalar_message(i, filters_s[i])
             if i >= LAG_V1:
-                filt_v1 = next_v1
-                if i - LAG_V1 + 1 < JT:
-                    next_v1 = filter_v1(i - LAG_V1 + 1)
-                gates_v1.append(vector_gate(i - LAG_V1, filt_v1))
-            if i == JT // 2:
+                jt = i - LAG_V1
+                if jt + 2 < JT:
+                    filters_v1.append(filter_v1(jt + 2))
+                gates_v1.append(vector_gate(jt, filters_v1[jt]))
+                if jt in (JT // 2, JT - 1):
+                    edges.append(edge_filter(len(edges)))
+            if i == LAG_V1:
                 quantise_w2_block(BLK_V2, w2_v2_chunks, 0)
 
-        sum_filter()
-        spent, gate = edge_filter(0)
-        for jh in range(F // BANK):
-            edge_gate(0, jh, spent, gate)
-        for i in range(ET):
-            if i + 1 < ET:
-                next_edge = edge_filter(i + 1)
-            for c in reversed(range(XD)):
-                vector_message(i, c, gates_v1[i], spent)
-                if c > 0:
-                    jh = XD - 1 - c
-                    if i + 1 < ET:
-                        edge_gate(i + 1, jh, *next_edge)
-                    sum_gate(i, jh, gate)
-            if i - 1 in products:
-                sum_product(i - 1)
-            spent, gate = next_edge
-        gate_sum = keep.tile([P, JT, XD], F32)
-        v2_rows = stage.tile([P, F], F32, tag="work", bufs=WORK_BUFS)
-        for jh in range(F // BANK):
-            nc.scalar.copy(out=v2_rows[:, jh * BANK : (jh + 1) * BANK], in_=v2_acc[jh][:])
-        for jh in range(F // BANK):
-            turn_ps = psum.tile([P, BANK // P, P], F32, tag="acc", bufs=2)
-            for k in range(BANK // P):
-                j0 = jh * BANK + k * P
-                nc.tensor.transpose(turn_ps[:, k, :], v2_rows[:, j0 : j0 + P], ident_f[:])
-            nc.vector.tensor_copy(
-                out=gate_sum[:, jh * (BANK // P) : (jh + 1) * (BANK // P), :], in_=turn_ps[:, :, 0:XD],
-            )
+        with tc.manual_schedule(engines={mybir.EngineType.Activation}):
+            spent, gate = edges[0]
+            for jh in range(F // BANK):
+                edge_gate(0, jh, spent, gate)
+            for i in range(ET):
+                if 1 < i + 1 < ET:
+                    edges.append(edge_filter(i + 1))
+                if i + 1 < ET:
+                    next_edge = edges[i + 1]
+                for c in reversed(range(XD)):
+                    vector_message(i, c, gates_v1[i], spent)
+                    if c > 0:
+                        jh = XD - 1 - c
+                        if i + 1 < ET:
+                            edge_gate(i + 1, jh, *next_edge)
+                        sum_gate(i, jh, gate)
+                if i - 1 in products:
+                    sum_product(i - 1)
+                if i == ET // 2:
+                    sum_filter()
+                spent, gate = next_edge
+            v2_rows = stage.tile([P, F], F32, tag="work", bufs=WORK_BUFS)
+            for jh in range(F // BANK):
+                nc.scalar.copy(out=v2_rows[:, jh * BANK : (jh + 1) * BANK], in_=v2_acc[jh][:])
+            for jh in range(F // BANK):
+                turn_ps = psum.tile([P, BANK // P, P], F32, tag="acc", bufs=2)
+                for k in range(BANK // P):
+                    j0 = jh * BANK + k * P
+                    nc.tensor.transpose(turn_ps[:, k, :], v2_rows[:, j0 : j0 + P], ident_f[:])
+                nc.vector.tensor_copy(
+                    out=terms_v2[:, jh * (BANK // P) : (jh + 1) * (BANK // P), PARTS, :], in_=turn_ps[:, :, 0:XD],
+                )
 
-        b2_cols = bias_cols[:, ROW_B2 + BLK_V2 * JT : ROW_B2 + (BLK_V2 + 1) * JT]
         res_v2 = keep.tile([P, JT, XD], F32)
-        nc.vector.tensor_tensor(
-            out=res_v2[:], in0=filt_sum[:], in1=b2_cols.unsqueeze(2).to_broadcast([P, JT, XD]), op=ALU.mult,
-        )
-        nc.vector.tensor_tensor(out=res_v2[:], in0=res_v2[:], in1=gate_sum[:], op=ALU.add)
+        nc.vector.tensor_reduce(out=res_v2[:], in_=terms_v2[:].rearrange("p j i c -> p j c i"), axis=AXIS_X, op=ALU.add)
         res = keep.tile([P, P], F32)
         nc.gpsimd.memset(res[:], 0.0)
         nc.vector.tensor_tensor(out=res[:, XD * JT : (XD + 1) * JT], in0=res_s[:, :, 0], in1=res_s[:, :, 1], op=ALU.add)

import math
from contextlib import ExitStack

import concourse.mybir as mybir
from concourse.masks import make_identity

BF16 = mybir.dt.bfloat16
F32 = mybir.dt.float32
U32 = mybir.dt.uint32
U8 = mybir.dt.uint8
FP8X4 = mybir.dt.float8_e4m3fn_x4
ALU = mybir.AluOpType
ACT = mybir.ActivationFunctionType
AXIS_X = mybir.AxisListType.X

P = 128
E = 1024
F = 1024
XD = 3
RC = 5.0
ET = E // P
JT = F // P
PACK = 4
K_PASS = P * PACK
PASSES = F // K_PASS
BANK = 512
HALVES = E // BANK
BLK_V1, BLK_S, BLK_V2 = 0, 1, 2
ROW_B2, ROW_BR, ROW_B1 = 0, 32, 64
PARTS = 3
VECTOR_SHARE = 344
GPSIMD_TILES = range(6)
RAW_BUFS = 3
GROUPED_BUFS = 4
RBF_BUFS = 5
WORK_BUFS = 12
GPSIMD_FILTERS_FROM = 3
AHEAD = 1
LAG_V1 = 2
TR_BUFS = 3
PHI_BUFS = 3

FLOPS = 2 * E * F * F + 2 * E * F * 3 * F


def regroup(nc, grouped, rows, vector_cols):
    width = rows.shape[2]
    dst = grouped.rearrange("p (c t) -> p c t", t=PACK)
    if vector_cols > 0:
        nc.vector.tensor_copy(
            out=dst[:, 0:vector_cols, :].rearrange("p (c i) t -> p c t i", i=4),
            in_=rows[:, :, 0:vector_cols].rearrange("p t (c i) -> p c t i", i=4),
        )
    if vector_cols < width:
        nc.scalar.copy(
            out=dst[:, vector_cols:width, :].rearrange("p (c i) t -> p c t i", i=4),
            in_=rows[:, :, vector_cols:width].rearrange("p t (c i) -> p c t i", i=4),
        )


def quantise(nc, grouped, codes, scales):
    nc.vector.quantize_mx(out=codes.bitcast(FP8X4), scales=scales, in_=grouped)


def split(nc, pool, name, value, parts, shape):
    rest = value
    for i, part in enumerate(parts):
        nc.gpsimd.tensor_copy(out=part, in_=rest)
        if i + 1 < len(parts):
            left = pool.tile(shape, F32, name="%s_rest%d" % (name, i))
            nc.gpsimd.tensor_tensor(out=left[:], in0=rest, in1=part, op=ALU.subtract)
            rest = left[:]


def mx_product(nc, acc, a_codes, a_scales, a_cols, b_codes, b_scales, b_cols):
    for g in range(PASSES):
        nc.tensor.matmul_mx(
            out=acc,
            lhsT=a_codes[:, g, a_cols].bitcast(FP8X4),
            lhsT_scale=a_scales[:, g, a_cols],
            rhs=b_codes[:, g, b_cols].bitcast(FP8X4),
            rhs_scale=b_scales[:, g, b_cols],
            start=(g == 0),
            stop=(g == PASSES - 1),
        )


def tile_message_pa_kernel(tc, s, r, v, rbf_proj, W1, b1, W2, b2, br, out_0, out_1):
    nc = tc.nc
    with ExitStack() as ctx:
        keep = ctx.enter_context(tc.tile_pool(name="keep", bufs=1))
        overlay = ctx.enter_context(tc.tile_pool(name="overlay", bufs=1))
        stage = ctx.enter_context(tc.tile_pool(name="stage", bufs=2))
        psum = ctx.enter_context(tc.psum_pool(name="psum", bufs=1))

        ident_f = keep.tile([P, P], F32)
        make_identity(nc, ident_f[:])
        ident_bf = keep.tile([P, P], BF16)
        make_identity(nc, ident_bf[:])

        r_bf = keep.tile([P, ET, XD], BF16)
        nc.sync.dma_start(out=r_bf[:], in_=r.rearrange("(p t) c -> p t c", t=ET))
        s_raw = overlay.tile([P, ET, F], BF16, offset=0)
        s_view = s.rearrange("(p t) k -> p t k", t=ET)
        EH = ET // HALVES

        def load_s_half(eh):
            nc.sync.dma_start(out=s_raw[:, eh * EH : (eh + 1) * EH, :], in_=s_view[:, eh * EH : (eh + 1) * EH, :])

        load_s_half(0)
        w1_raw = []
        for g in range(PASSES):
            raw = stage.tile([P, PACK, F], BF16, tag="raw", bufs=RAW_BUFS)
            nc.sync.dma_start(
                out=raw[:].rearrange("q (u e) c -> q u (e c)", u=2),
                in_=W1[g * K_PASS : (g + 1) * K_PASS, :].rearrange("(u q e) c -> q u (e c)", u=2, e=2),
            )
            w1_raw.append(raw)
        load_s_half(1)
        bias_rows = keep.tile([P, P], BF16)
        nc.gpsimd.memset(bias_rows[:], 0.0)
        nc.sync.dma_start(out=bias_rows[ROW_B2 : ROW_B2 + 3 * JT, :], in_=b2.rearrange("(a c) -> a c", c=P))
        nc.sync.dma_start(out=bias_rows[ROW_BR : ROW_BR + 3 * JT, :], in_=br.rearrange("(a c) -> a c", c=P))
        nc.sync.dma_start(out=bias_rows[ROW_B1 : ROW_B1 + JT, :], in_=b1.rearrange("(a c) -> a c", c=P))

        def load_w2_block(blk):
            chunks = []
            for g in range(PASSES):
                raw = stage.tile([P, PACK, F], BF16, tag="raw", bufs=RAW_BUFS)
                nc.sync.dma_start(
                    out=raw[:],
                    in_=W2[g * K_PASS : (g + 1) * K_PASS, blk * F : (blk + 1) * F].rearrange("(t p) n -> p t n", p=P),
                )
                chunks.append(raw)
            return chunks

        def load_rbf_block(blk):
            halves = []
            for half in range(HALVES):
                rbf = stage.tile([P, EH, F], BF16, tag="rbf", bufs=RBF_BUFS)
                nc.sync.dma_start(
                    out=rbf[:],
                    in_=rbf_proj[:, blk * F : (blk + 1) * F].rearrange("(p t) j -> p t j", t=ET)[:, half * EH : (half + 1) * EH, :],
                )
                halves.append(rbf)
            return halves

        h_lin = overlay.tile([P, PASSES, PACK, E], BF16, offset=16384)
        s_codes = overlay.tile([P, PASSES, E], U32, offset=32768, align_bytes=64)
        w1_codes = overlay.tile([P, PASSES, F], U32, offset=40960, align_bytes=64)
        s_scales = overlay.tile([P, PASSES, E], U8, offset=49152, align_bytes=64)
        w1_scales = overlay.tile([P, PASSES, F], U8, offset=51200, align_bytes=64)
        h_codes = keep.tile([P, PASSES, E], U32, align_bytes=64)
        h_scales = keep.tile([P, PASSES, E], U8, align_bytes=64)
        w2_codes = keep.tile([P, PASSES, 3 * F], U32, align_bytes=64)
        w2_scales = keep.tile([P, PASSES, 3 * F], U8, align_bytes=64)

        w2_s_chunks = load_w2_block(BLK_S)
        rbf_s = load_rbf_block(BLK_S)
        w2_v1_chunks = load_w2_block(BLK_V1)
        rbf_v1 = load_rbf_block(BLK_V1)
        br_bc = keep.tile([P, F], BF16)
        nc.sync.dma_start(out=br_bc[:], in_=br[BLK_V2 * F : (BLK_V2 + 1) * F].partition_broadcast(P))

        def quantise_weights(chunks, codes, scales, col0, vector_cols):
            for c0 in range(0, F, BANK):
                for g in range(PASSES):
                    grouped = stage.tile([P, PACK * BANK], BF16, tag="grouped", bufs=GROUPED_BUFS, align_bytes=64)
                    regroup(nc, grouped[:], chunks[g][:, :, c0 : c0 + BANK], vector_cols)
                    cols = slice(col0 + c0, col0 + c0 + BANK)
                    quantise(nc, grouped[:], codes[:, g, cols], scales[:, g, cols])

        def quantise_w2_block(blk, chunks, vector_cols):
            quantise_weights(chunks, w2_codes, w2_scales, blk * F, vector_cols)

        s_words = s_raw[:].bitcast(F32)

        def quantise_s_half(eh):
            grouped = []
            for g in range(PASSES):
                tile_g = stage.tile([P, PACK * BANK], BF16, tag="grouped", bufs=GROUPED_BUFS, align_bytes=64, name="s_grouped%d" % g)
                grouped.append(tile_g)
            for tp in range(EH // 2):
                for g in range(PASSES):
                    s_ps = psum.tile([P, 2, 2 * P], F32, tag="tr", bufs=TR_BUFS)
                    for u in range(2):
                        for i in range(2):
                            w0 = g * (K_PASS // 2) + u * P
                            nc.tensor.transpose(
                                s_ps[:, u, i * P : (i + 1) * P], s_words[:, eh * EH + 2 * tp + i, w0 : w0 + P], ident_f[:]
                            )
                    dst = grouped[g][:].bitcast(F32).rearrange("p (e u) -> p e u", u=2)
                    dst = dst[:, tp * 2 * P : (tp + 1) * 2 * P, :]
                    if g == 0 and eh == 0:
                        nc.vector.tensor_copy(out=dst, in_=s_ps[:].rearrange("p u e -> p e u"))
                    else:
                        nc.scalar.copy(out=dst, in_=s_ps[:].rearrange("p u e -> p e u"))
            edges = slice(eh * BANK, (eh + 1) * BANK)
            for g in range(PASSES):
                quantise(nc, grouped[g][:], s_codes[:, g, edges], s_scales[:, g, edges])

        def first_product(eh):
            edges = slice(eh * BANK, (eh + 1) * BANK)
            for g2 in range(PASSES):
                for t in range(PACK):
                    ft = g2 * PACK + t
                    h_ps = psum.tile([P, BANK], F32, tag="phi", bufs=PHI_BUFS)
                    mx_product(nc, h_ps[:], w1_codes, w1_scales, slice(ft * P, (ft + 1) * P), s_codes, s_scales, edges)
                    nc.scalar.activation(
                        out=h_lin[:, g2, t, edges], in_=h_ps[:], func=ACT.Silu,
                        bias=bias_cols[:, ROW_B1 + ft : ROW_B1 + ft + 1], scale=1.0,
                    )
                grouped = stage.tile([P, PACK * BANK], BF16, tag="grouped", bufs=GROUPED_BUFS, align_bytes=64)
                regroup(nc, grouped[:], h_lin[:, g2, :, edges], BANK)
                quantise(nc, grouped[:], h_codes[:, g2, edges], h_scales[:, g2, edges])

        r32 = keep.tile([P, ET, XD], F32)
        nc.gpsimd.tensor_copy(out=r32[:], in_=r_bf[:])
        r_sq = keep.tile([P, ET, XD], F32)
        nc.gpsimd.tensor_tensor(out=r_sq[:], in0=r32[:], in1=r32[:], op=ALU.mult)
        d_sq = keep.tile([P, ET], F32)
        nc.gpsimd.tensor_tensor(out=d_sq[:], in0=r_sq[:, :, 0], in1=r_sq[:, :, 1], op=ALU.add)
        nc.gpsimd.tensor_tensor(out=d_sq[:], in0=d_sq[:], in1=r_sq[:, :, 2], op=ALU.add)
        dist = keep.tile([P, ET], F32)
        nc.scalar.activation(out=dist[:], in_=d_sq[:], func=ACT.Sqrt)
        inv_d = keep.tile([P, ET], F32)
        nc.vector.reciprocal(out=inv_d[:], in_=dist[:])
        d_clip = keep.tile([P, ET], F32)
        nc.gpsimd.tensor_scalar_min(out=d_clip[:], in0=dist[:], scalar1=RC)
        sin_d = keep.tile([P, ET], F32)
        nc.scalar.activation(out=sin_d[:], in_=d_clip[:], func=ACT.Sin, scale=math.pi / (2.0 * RC))
        silu_warm = keep.tile([P, 1], F32)
        nc.scalar.activation(out=silu_warm[:], in_=sin_d[:, 0:1], func=ACT.Silu)
        inside = keep.tile([P, ET], F32)
        nc.gpsimd.tensor_single_scalar(out=inside[:], in_=dist[:], scalar=RC, op=ALU.is_lt)
        sin_sq = keep.tile([P, ET], F32)
        nc.gpsimd.tensor_tensor(out=sin_sq[:], in0=sin_d[:], in1=sin_d[:], op=ALU.mult)
        cos_sq = keep.tile([P, ET], F32)
        nc.gpsimd.tensor_scalar(out=cos_sq[:], in0=sin_sq[:], scalar1=-1.0, scalar2=1.0, op0=ALU.mult, op1=ALU.add)
        fcut = keep.tile([P, ET], F32)
        nc.gpsimd.tensor_tensor(out=fcut[:], in0=cos_sq[:], in1=inside[:], op=ALU.mult)
        fcut_over_d = keep.tile([P, ET], F32)
        nc.gpsimd.tensor_tensor(out=fcut_over_d[:], in0=fcut[:], in1=inv_d[:], op=ALU.mult)
        edge_w = keep.tile([P, ET, P], F32)
        nc.gpsimd.memset(edge_w[:], 0.0)
        weights = keep.tile([P, ET, XD], F32)
        nc.gpsimd.tensor_tensor(
            out=weights[:], in0=r32[:], in1=fcut_over_d[:].unsqueeze(2).to_broadcast([P, ET, XD]), op=ALU.mult,
        )
        nc.gpsimd.tensor_copy(out=edge_w[:, :, 0:XD], in_=weights[:])
        weight_sum = keep.tile([P, XD], F32)
        nc.vector.tensor_reduce(out=weight_sum[:], in_=weights[:].rearrange("p t c -> p c t"), axis=AXIS_X, op=ALU.add)
        w_parts = keep.tile([P, ET, PARTS, XD], BF16)
        w_sum_parts = keep.tile([P, PARTS, XD], BF16)
        split(nc, keep, "w", weights[:], [w_parts[:, :, i, :] for i in range(PARTS)], [P, ET, XD])
        split(nc, keep, "ws", weight_sum[:], [w_sum_parts[:, i, :] for i in range(PARTS)], [P, XD])

        quantise_s_half(0)
        quantise_weights(w1_raw, w1_codes, w1_scales, 0, VECTOR_SHARE)
        bias_ps = psum.tile([P, P], BF16, tag="tr", bufs=TR_BUFS)
        nc.tensor.transpose(bias_ps[:], bias_rows[:], ident_bf[:])
        bias_cols = keep.tile([P, P], F32)
        nc.scalar.copy(out=bias_cols[:], in_=bias_ps[:])

        quantise_s_half(1)
        first_product(0)
        fcut_bc = keep.tile([P, E], F32)
        for eh in range(HALVES):
            rep_ps = psum.tile([P, BANK], F32, tag="tr", bufs=TR_BUFS)
            for i in range(EH):
                nc.tensor.transpose(
                    rep_ps[:, i * P : (i + 1) * P], fcut[:, eh * EH + i : eh * EH + i + 1].to_broadcast([P, P]), ident_f[:]
                )
            nc.scalar.copy(out=fcut_bc[:, eh * BANK : (eh + 1) * BANK], in_=rep_ps[:])
        quantise_w2_block(BLK_S, w2_s_chunks, VECTOR_SHARE)
        def turned_rbf(jt, rbf):
            rbf_ps = psum.tile([P, E], BF16, tag="tr", bufs=TR_BUFS)
            for t in range(ET):
                nc.tensor.transpose(rbf_ps[:, t * P : (t + 1) * P], rbf[t // EH][:, t % EH, jt * P : (jt + 1) * P], ident_bf[:])
            return rbf_ps

        def filter_s(jt):
            rbf_ps = turned_rbf(jt, rbf_s)
            filt = stage.tile([P, E], F32, tag="work", bufs=WORK_BUFS, name="filt_s")
            col = ROW_BR + BLK_S * JT + jt
            nc.vector.scalar_tensor_tensor(
                out=filt[:], in0=rbf_ps[:], scalar=bias_cols[:, col : col + 1], in1=fcut_bc[:], op0=ALU.add, op1=ALU.mult,
            )
            return filt

        def filter_v1(jt):
            rbf_ps = turned_rbf(jt, rbf_v1)
            filt = stage.tile([P, E], F32, tag="work", bufs=WORK_BUFS, name="filt_v1")
            col = ROW_BR + BLK_V1 * JT + jt
            if jt < GPSIMD_FILTERS_FROM:
                nc.vector.scalar_tensor_tensor(
                    out=filt[:], in0=rbf_ps[:], scalar=bias_cols[:, col : col + 1], in1=fcut_bc[:], op0=ALU.add, op1=ALU.mult,
                )
            else:
                nc.scalar.activation(out=filt[:], in_=rbf_ps[:], func=ACT.Identity, bias=bias_cols[:, col : col + 1], scale=1.0)
                nc.gpsimd.tensor_tensor(out=filt[:], in0=filt[:], in1=fcut_bc[:], op=ALU.mult)
            return filt

        first_product(1)
        quantise_w2_block(BLK_V1, w2_v1_chunks, 0)

        w2_v2_chunks = load_w2_block(BLK_V2)
        v_view = v.rearrange("(p t) c j -> p t c j", t=ET)
        v_sb = []
        for a in range(0, ET, 2):
            v_pair = overlay.tile([P, 2, XD, F], BF16, offset=(a // 2) * 12288, name="v_pair%d" % a)
            nc.sync.dma_start(out=v_pair[:], in_=v_view[:, a : a + 2])
            v_sb.append(v_pair)
        rbf_v2 = load_rbf_block(BLK_V2)

        terms_v2 = keep.tile([P, JT, PARTS + 1, XD], F32)
        v2_acc = []
        for jh in range(F // BANK):
            acc = psum.tile([P, BANK], F32, tag="acc", bufs=2, name="v2_acc%d" % jh)
            v2_acc.append(acc)

        def sum_filter():
            filt_ps = psum.tile([P, JT, PARTS, XD], F32, tag="tr", bufs=TR_BUFS)
            for jt in range(JT):
                cols = slice(jt * P, (jt + 1) * P)
                for t in range(ET):
                    nc.tensor.matmul(
                        out=filt_ps[:, jt], lhsT=rbf_v2[t // EH][:, t % EH, cols], rhs=w_parts[:, t], start=(t == 0), stop=False
                    )
                nc.tensor.matmul(out=filt_ps[:, jt], lhsT=br_bc[:, cols], rhs=w_sum_parts[:], start=False, stop=True)
            for jt in range(JT):
                col = ROW_B2 + BLK_V2 * JT + jt
                nc.scalar.activation(
                    out=terms_v2[:, jt, 0:PARTS, :], in_=filt_ps[:, jt], func=ACT.Copy, scale=bias_cols[:, col : col + 1],
                )

        def edge_filter(t):
            filt = stage.tile([P, F], F32, tag="work", bufs=WORK_BUFS, name="edge_filt")
            nc.gpsimd.tensor_tensor(out=filt[:], in0=rbf_v2[t // EH][:, t % EH, :], in1=br_bc[:], op=ALU.add)
            gate = stage.tile([P, F], F32, tag="work", bufs=WORK_BUFS, name="edge_gate")
            return filt, gate

        def edge_gate(t, jh, filt, gate):
            cols = slice(jh * BANK, (jh + 1) * BANK)
            phi_ps = psum.tile([P, BANK], F32, tag="phi", bufs=PHI_BUFS)
            mx_product(
                nc, phi_ps[:], h_codes, h_scales, slice(t * P, (t + 1) * P),
                w2_codes, w2_scales, slice(BLK_V2 * F + jh * BANK, BLK_V2 * F + (jh + 1) * BANK),
            )
            nc.vector.tensor_tensor(out=gate[:, cols], in0=phi_ps[:], in1=filt[:, cols], op=ALU.mult)

        def sum_gate(t, jh, gate):
            nc.tensor.matmul(
                out=v2_acc[jh][:], lhsT=edge_w[:, t, :], rhs=gate[:, jh * BANK : (jh + 1) * BANK],
                start=(t == 0), stop=(t == ET - 1),
            )

        def phi_tile(blk, jt, eh):
            phi_ps = psum.tile([P, BANK], F32, tag="phi", bufs=PHI_BUFS)
            j0 = blk * F + jt * P
            mx_product(
                nc, phi_ps[:], w2_codes, w2_scales, slice(j0, j0 + P),
                h_codes, h_scales, slice(eh * BANK, (eh + 1) * BANK),
            )
            return phi_ps

        res_s = keep.tile([P, JT, HALVES], F32)
        res_v1 = keep.tile([P, XD, JT], F32)

        def scalar_message(jt, filt):
            col = ROW_B2 + BLK_S * JT + jt
            for eh in range(HALVES):
                phi_ps = phi_tile(BLK_S, jt, eh)
                nc.vector.scalar_tensor_tensor(
                    out=filt[:, eh * BANK : (eh + 1) * BANK], in0=phi_ps[:], scalar=bias_cols[:, col : col + 1],
                    in1=filt[:, eh * BANK : (eh + 1) * BANK], op0=ALU.add, op1=ALU.mult,
                    accum_out=res_s[:, jt, eh : eh + 1],
                )

        def vector_gate(jt, filt):
            col = ROW_B2 + BLK_V1 * JT + jt
            gate = stage.tile([P, E], F32, tag="work", bufs=WORK_BUFS, name="vector_gate")
            for eh in range(HALVES):
                edges = slice(eh * BANK, (eh + 1) * BANK)
                phi_ps = phi_tile(BLK_V1, jt, eh)
                nc.vector.scalar_tensor_tensor(
                    out=gate[:, edges], in0=phi_ps[:], scalar=bias_cols[:, col : col + 1],
                    in1=filt[:, edges], op0=ALU.add, op1=ALU.mult,
                )
            return gate

        def vector_message(jt, c, gate, spent):
            on_gpsimd = c == XD - 1 and jt in GPSIMD_TILES
            v_ps = psum.tile([P, E], BF16, tag="tr", bufs=TR_BUFS)
            for t in range(ET):
                nc.tensor.transpose(v_ps[:, t * P : (t + 1) * P], v_sb[t // 2][:, t % 2, c, jt * P : (jt + 1) * P], ident_bf[:])
            if on_gpsimd:
                product = stage.tile([P, E], F32, tag="raw", bufs=RAW_BUFS, name="product")
                v_copy = stage.tile([P, E], BF16, tag="grouped", bufs=GROUPED_BUFS, align_bytes=64, name="v_copy")
                nc.scalar.copy(out=v_copy[:], in_=v_ps[:])
                nc.gpsimd.tensor_tensor(out=product[:], in0=gate[:], in1=v_copy[:], op=ALU.mult)
                products[jt] = product
            else:
                nc.vector.scalar_tensor_tensor(
                    out=spent[:], in0=v_ps[:], scalar=1.0, in1=gate[:], op0=ALU.mult, op1=ALU.mult,
                    accum_out=res_v1[:, c, jt : jt + 1],
                )

        products = {}

        def sum_product(jt):
            nc.scalar.activation(
                out=products[jt][:], in_=products[jt][:], func=ACT.Identity, accum_out=res_v1[:, XD - 1, jt : jt + 1],
            )

        gates_v1 = []
        edges = []
        filters_s = [filter_s(jt) for jt in range(AHEAD)]
        filters_v1 = [filter_v1(0), filter_v1(1)]
        for i in range(JT + LAG_V1):
            if i + AHEAD < JT:
                filters_s.append(filter_s(i + AHEAD))
            if i < JT:
                scalar_message(i, filters_s[i])
            if i >= LAG_V1:
                jt = i - LAG_V1
                if jt + 2 < JT:
                    filters_v1.append(filter_v1(jt + 2))
                gates_v1.append(vector_gate(jt, filters_v1[jt]))
                if jt in (JT // 2, JT - 1):
                    edges.append(edge_filter(len(edges)))
            if i == LAG_V1:
                quantise_w2_block(BLK_V2, w2_v2_chunks, 0)

        with tc.manual_schedule(engines={mybir.EngineType.Activation}):
            spent, gate = edges[0]
            for jh in range(F // BANK):
                edge_gate(0, jh, spent, gate)
            for i in range(ET):
                if 1 < i + 1 < ET:
                    edges.append(edge_filter(i + 1))
                if i + 1 < ET:
                    next_edge = edges[i + 1]
                for c in reversed(range(XD)):
                    vector_message(i, c, gates_v1[i], spent)
                    if c > 0:
                        jh = XD - 1 - c
                        if i + 1 < ET:
                            edge_gate(i + 1, jh, *next_edge)
                        sum_gate(i, jh, gate)
                if i - 1 in products:
                    sum_product(i - 1)
                if i == ET // 2:
                    sum_filter()
                spent, gate = next_edge
            v2_rows = stage.tile([P, F], F32, tag="work", bufs=WORK_BUFS)
            for jh in range(F // BANK):
                nc.scalar.copy(out=v2_rows[:, jh * BANK : (jh + 1) * BANK], in_=v2_acc[jh][:])
            for jh in range(F // BANK):
                turn_ps = psum.tile([P, BANK // P, P], F32, tag="acc", bufs=2)
                for k in range(BANK // P):
                    j0 = jh * BANK + k * P
                    nc.tensor.transpose(turn_ps[:, k, :], v2_rows[:, j0 : j0 + P], ident_f[:])
                nc.vector.tensor_copy(
                    out=terms_v2[:, jh * (BANK // P) : (jh + 1) * (BANK // P), PARTS, :], in_=turn_ps[:, :, 0:XD],
                )

        res_v2 = keep.tile([P, JT, XD], F32)
        nc.vector.tensor_reduce(out=res_v2[:], in_=terms_v2[:].rearrange("p j i c -> p j c i"), axis=AXIS_X, op=ALU.add)
        res = keep.tile([P, P], F32)
        nc.gpsimd.memset(res[:], 0.0)
        nc.vector.tensor_tensor(out=res[:, XD * JT : (XD + 1) * JT], in0=res_s[:, :, 0], in1=res_s[:, :, 1], op=ALU.add)
        nc.vector.tensor_tensor(
            out=res[:, 0 : XD * JT].rearrange("p (c j) -> p c j", c=XD), in0=res_v1[:],
            in1=res_v2[:].rearrange("p j c -> p c j"), op=ALU.add,
        )
        res_ps = psum.tile([P, P], F32, tag="tr", bufs=TR_BUFS)
        nc.tensor.transpose(res_ps[:], res[:], ident_f[:])
        res_rows = keep.tile([P, P], F32)
        nc.vector.tensor_copy(out=res_rows[:], in_=res_ps[:])
        nc.sync.dma_start(out=out_0.rearrange("c (j p) -> (c j) p", p=P), in_=res_rows[0 : XD * JT, :])
        nc.sync.dma_start(out=out_1.rearrange("(j p) -> j p", p=P), in_=res_rows[XD * JT : (XD + 1) * JT, :])
